import numpy as np
import ml_dtypes


def mxq(x, axis, fmt="e4m3"):
    dtype, down = {"e4m3": (ml_dtypes.float8_e4m3fn, 7), "e5m2": (ml_dtypes.float8_e5m2, 14)}[fmt]
    v = np.moveaxis(np.asarray(x, np.float32).astype(ml_dtypes.bfloat16).astype(np.float64), axis, -1)
    blocks = v.reshape(v.shape[:-1] + (-1, 32))
    amax = np.abs(blocks).max(-1, keepdims=True)
    byte = np.maximum(np.where(amax > 0, np.frexp(amax)[1] - 1 + 127, 0) - down, 1)
    scale = np.exp2(byte - 127.0)
    codes = (blocks / scale).astype(np.float32).astype(dtype).astype(np.float64)
    return np.moveaxis((codes * scale).reshape(v.shape), -1, axis)


WIDE = False


def mx_kscale(k):
    if not WIDE:
        return np.ones(k)
    levels = np.array([10, -10, 5, -5, 0])
    a = np.random.permutation(np.resize(levels, k // 512 * 4)).reshape(k // 512, 4)
    idx = np.arange(k)
    return np.exp2(a[idx // 512, idx % 128 // 32])


BF16 = ml_dtypes.bfloat16


def bf(x):
    return np.asarray(x, np.float32).astype(BF16)


def f64(x):
    return np.asarray(x).astype(np.float64)


E2M1 = np.array([0.0, 0.5, 1.0, 1.5, 2.0, 3.0, 4.0, 6.0, -0.0, -0.5, -1.0, -1.5, -2.0, -3.0, -4.0, -6.0])


def pack_weight(w, fmt):
    k, n = w.shape
    w = f64(bf(w)).reshape(k // 32, 32, n)
    amax = np.abs(w).max(1)
    if fmt == "e4m3":
        byte = np.frexp(amax)[1] - 1 + 127 - 7
    else:
        mant, ex = np.frexp(amax / 6.0)
        byte = np.where(mant > 0.5, ex, ex - 1) + 127
    byte = np.clip(np.where(amax > 0, byte, 1), 1, 254)
    scaled = (w * np.exp2(127.0 - byte)[:, None, :]).reshape(k, n).astype(np.float32)
    by_word = np.ascontiguousarray(scaled.reshape(k // 512, 128, 4, n).transpose(0, 1, 3, 2))
    if fmt == "e4m3":
        words = by_word.astype(ml_dtypes.float8_e4m3fn).view(np.uint8)
    else:
        c = by_word.astype(ml_dtypes.float4_e2m1fn).view(np.uint8) & 0xF
        words = c[..., 0::2] | (c[..., 1::2] << 4)
    return np.ascontiguousarray(words), np.ascontiguousarray(byte.astype(np.uint8).reshape(k // 512, 16, n))


def unpack_weight(words, scales, fmt):
    g, p, n, _ = words.shape
    if fmt == "e4m3":
        vals = np.ascontiguousarray(words).view(ml_dtypes.float8_e4m3fn).astype(np.float64)
    else:
        nib = np.empty((g, p, n, 4), np.uint8)
        nib[..., 0::2] = words & 0xF
        nib[..., 1::2] = words >> 4
        vals = E2M1[nib]
    vals = vals * np.repeat(np.exp2(scales.astype(np.float64) - 127.0), 8, axis=1)[..., None]
    return vals.transpose(0, 1, 3, 2).reshape(g * 512, n)


B, D, O1, O2, O3 = 1024, 1536, 1024, 512, 128
EPS = 1e-5
FMT = "e4m3"


def mish(v):
    return v * np.tanh(np.log(1.0 + np.exp(v)))


def sigmoid(v):
    return 1.0 / (1.0 + np.exp(-v))


def ln(u, g, b):
    mu = u.mean(-1, keepdims=True)
    var = np.square(u - mu).mean(-1, keepdims=True)
    return (u - mu) * (1.0 / np.sqrt(var + EPS)) * g + b


def setup_inputs():
    s = mx_kscale(O2)
    h_dec1 = bf(mish(np.random.standard_normal((B, O2))) * s)
    d2 = np.random.standard_normal((O1, O2)) * 1.5 / np.sqrt(O2) / s
    D2_words, D2_scales = pack_weight(np.ascontiguousarray(d2.T), FMT)
    g4 = bf(1.0 + 0.1 * np.random.standard_normal(O1))
    b4 = bf(0.1 * np.random.standard_normal(O1))
    d3 = np.random.standard_normal((D, O1)) * 1.5 / np.sqrt(O1)
    D3_words, D3_scales = pack_weight(np.ascontiguousarray(d3.T), FMT)
    bo = bf(0.3 * np.random.standard_normal(D))
    return {"h_dec1": h_dec1,
            "D2_words": D2_words,
            "D2_scales": D2_scales,
            "g4": g4,
            "b4": b4,
            "D3_words": D3_words,
            "D3_scales": D3_scales,
            "bo": bo}


def reference(h_dec1, D2_words, D2_scales, g4, b4, D3_words, D3_scales, bo):
    u = mxq(f64(h_dec1), 1, "e4m3") @ unpack_weight(D2_words, D2_scales, FMT)
    h = mish(ln(u, f64(g4), f64(b4)))
    return sigmoid((mxq(h, 1, "e4m3") @ unpack_weight(D3_words, D3_scales, FMT)) + f64(bo))

@@ -1,0 +1,273 @@
+from contextlib import ExitStack
+
+import concourse.mybir as mybir
+from concourse.masks import make_identity
+
+F32 = mybir.dt.float32
+BF16 = mybir.dt.bfloat16
+I32 = mybir.dt.int32
+U32 = mybir.dt.uint32
+U8 = mybir.dt.uint8
+FP8X4 = mybir.dt.float8_e4m3fn_x4
+ACT = mybir.ActivationFunctionType
+ALU = mybir.AluOpType
+
+P = 128
+PACK = 4
+K_PASS = P * PACK
+BANK = 512
+
+BATCH, D_IN, D_HID, D_OUT = 1024, 512, 1024, 1536
+TILES = BATCH // P
+HID_BANKS = D_HID // BANK
+HID_PASSES = D_HID // K_PASS
+ROUND = 4
+EPS = 1e-5
+LN_FLOOR = 2.0**-60
+
+FLOPS = 2 * BATCH * D_IN * D_HID + 2 * BATCH * D_HID * D_OUT
+
+
+def tile_autoencoder_pb_kernel(tc, h_dec1, D2_words, D2_scales, g4, b4, D3_words, D3_scales, bo, out):
+    nc = tc.nc
+    with ExitStack() as stack:
+        stack.enter_context(tc.manual_schedule())
+        keep = stack.enter_context(tc.tile_pool(name="keep", bufs=1))
+        small = stack.enter_context(tc.tile_pool(name="small", bufs=4))
+        rows = stack.enter_context(tc.tile_pool(name="rows", bufs=TILES))
+        work = stack.enter_context(tc.tile_pool(name="work", bufs=2))
+        result = stack.enter_context(tc.tile_pool(name="result", bufs=4))
+        psum = stack.enter_context(tc.psum_pool(name="psum", bufs=8))
+
+        planes = keep.tile([P, D_OUT], U8, align_bytes=64)
+        nc.vector.memset(planes[:].bitcast(I32), 0)
+        D2_PLANE = 2 * PACK
+        GAIN, SHIFT, OUT_BIAS = 0, D_HID, 2 * D_HID
+        vectors = keep.tile([P, 2 * D_HID + D_OUT], BF16)
+        nc.vector.memset(vectors[:], 0.0)
+        ones = keep.tile([P, P], BF16)
+        nc.vector.memset(ones[:], 1.0)
+        ln_floor = keep.tile([P, 1], F32)
+        nc.vector.memset(ln_floor[:], LN_FLOOR)
+        minus_half = keep.tile([P, 1], F32)
+        nc.vector.memset(minus_half[:], -0.5)
+        ident = keep.tile([P, P], F32)
+        make_identity(nc, ident[:])
+        warm = keep.tile([P, 1], F32)
+        nc.scalar.activation(out=warm[:], in_=ln_floor[:], func=ACT.Sigmoid)
+
+        x_sb = keep.tile([P, TILES, D_IN], BF16)
+        x_rows = h_dec1.rearrange("(i p) k -> p i k", p=P)
+        w2_words = keep.tile([P, D_HID], U32, align_bytes=64)
+        w3_words = keep.tile([P, HID_PASSES, D_OUT], U32, align_bytes=64)
+        nc.sync.dma_start(out=x_sb[:, 0:2, :], in_=x_rows[:, 0:2, :])
+        for quad in range(4):
+            nc.sync.dma_start(
+                out=planes[32 * quad + D2_PLANE : 32 * quad + D2_PLANE + 4, 0:D_HID].bitcast(I32),
+                in_=D2_scales[0, 4 * quad : 4 * quad + 4, :].bitcast(I32),
+            )
+        nc.sync.dma_start(
+            out=w2_words[:].bitcast(I32), in_=D2_words[0].rearrange("p n t -> p (n t)").bitcast(I32)
+        )
+        nc.scalar.dma_start(out=vectors[0:1, GAIN : GAIN + D_HID], in_=g4.unsqueeze(0))
+        nc.scalar.dma_start(out=vectors[0:1, SHIFT : SHIFT + D_HID], in_=b4.unsqueeze(0))
+        nc.scalar.dma_start(out=vectors[0:1, OUT_BIAS : OUT_BIAS + D_OUT], in_=bo.unsqueeze(0))
+        nc.sync.dma_start(out=x_sb[:, 2:TILES, :], in_=x_rows[:, 2:TILES, :])
+        for quad in range(4):
+            nc.sync.dma_start(
+                out=planes[32 * quad : 32 * quad + 4 * HID_PASSES, :].bitcast(I32),
+                in_=D3_scales[:, 4 * quad : 4 * quad + 4, :].bitcast(I32),
+            )
+        for g in range(HID_PASSES):
+            nc.sync.dma_start(
+                out=w3_words[:, g, :].bitcast(I32),
+                in_=D3_words[g].rearrange("p n t -> p (n t)").bitcast(I32),
+            )
+
+        spread = keep.tile([P, 2 * D_HID + D_OUT], BF16)
+
+        def spread_vectors(first_col, width):
+            for col in range(first_col, first_col + width, BANK):
+                summed = psum.tile([P, BANK], F32, tag="bank")
+                nc.tensor.matmul(
+                    out=summed[:], lhsT=ones[:], rhs=vectors[:, col : col + BANK], start=True, stop=True
+                )
+                nc.scalar.copy(out=spread[:, col : col + BANK], in_=summed[:])
+
+        x_grouped = keep.tile([P, TILES, P, PACK], BF16, align_bytes=64)
+        x_codes = keep.tile([P, TILES * P], U32, align_bytes=64)
+        x_scales = keep.tile([P, TILES * P], U8, align_bytes=64)
+
+        def x_pair(c):
+            return x_grouped[:, 2 * c : 2 * c + 2, :, :].rearrange("p i b t -> p (i b t)")
+
+        def transpose_x(c):
+            x_t = psum.tile([P, 2, 2, P], F32, tag="bank")
+            for i in range(2):
+                words = x_sb[:, 2 * c + i, :].bitcast(F32)
+                for half in range(2):
+                    nc.tensor.transpose(x_t[:, i, half, :], words[:, half : D_IN // 2 : 2], ident[:])
+            nc.scalar.copy(
+                out=x_pair(c).bitcast(F32).rearrange("p (i b h) -> p i b h", i=2, h=2),
+                in_=x_t[:].rearrange("p i h b -> p i b h"),
+            )
+
+        def quantise_x(c):
+            cols = slice(2 * c * P, (2 * c + 2) * P)
+            nc.vector.quantize_mx(out=x_codes[:, cols].bitcast(FP8X4), scales=x_scales[:, cols], in_=x_pair(c))
+
+        u_of = {}
+        y_of = {}
+        t_of = {}
+        h_of = {}
+        codes_of = {}
+
+        def first_matmul(i):
+            batch = slice(i * P, (i + 1) * P)
+            u_of[i] = []
+            for j in range(HID_BANKS):
+                cols = slice(j * BANK, (j + 1) * BANK)
+                u = psum.tile([P, BANK], F32, tag="bank")
+                nc.tensor.matmul_mx(
+                    out=u[:],
+                    lhsT=x_codes[:, batch].bitcast(FP8X4),
+                    lhsT_scale=x_scales[:, batch],
+                    rhs=w2_words[:, cols].bitcast(FP8X4),
+                    rhs_scale=planes[D2_PLANE:P, cols],
+                    start=True,
+                    stop=True,
+                )
+                u_of[i].append(u)
+
+        def layer_norm(i):
+            stats = small.tile([P, HID_BANKS, 6], F32)
+            for j in range(HID_BANKS):
+                nc.vector.bn_stats(out=stats[:, j, :], in_=u_of[i][j][:])
+            mean_var = small.tile([P, 2], F32)
+            nc.vector.bn_aggr(out=mean_var[:], in_=stats[:].rearrange("p j s -> p (j s)"))
+            var_eps = small.tile([P, 1], F32)
+            nc.gpsimd.tensor_scalar(
+                out=var_eps[:], in0=mean_var[:, 1:2], scalar1=1.0, scalar2=EPS, op0=ALU.mult, op1=ALU.add
+            )
+            rstd = small.tile([P, 1], F32)
+            nc.gpsimd.tensor_tensor(out=rstd[:], in0=var_eps[:], in1=minus_half[:], op=ALU.pow)
+            centred = work.tile([P, D_HID], F32)
+            for j in range(HID_BANKS):
+                cols = slice(j * BANK, (j + 1) * BANK)
+                nc.vector.scalar_tensor_tensor(
+                    out=centred[:, cols],
+                    in0=u_of[i][j][:],
+                    scalar=mean_var[:, 0:1],
+                    in1=spread[:, GAIN + j * BANK : GAIN + (j + 1) * BANK],
+                    op0=ALU.subtract,
+                    op1=ALU.mult,
+                )
+            y = rows.tile([P, D_HID], F32)
+            nc.vector.scalar_tensor_tensor(
+                out=y[:],
+                in0=centred[:],
+                scalar=rstd[:],
+                in1=spread[:, SHIFT : SHIFT + D_HID],
+                op0=ALU.mult,
+                op1=ALU.add,
+            )
+            y_of[i] = y
+
+        def first_layer(i):
+            layer_norm(i)
+            if i + 2 < TILES:
+                if i % 2 == 0:
+                    quantise_x(i // 2 + 1)
+                first_matmul(i + 2)
+
+        def mish_sigmoid(i):
+            t = rows.tile([P, D_HID], F32)
+            nc.scalar.activation(out=t[:], in_=y_of[i][:], func=ACT.Sigmoid, scale=-1.0)
+            t_of[i] = t
+
+        def mish_ln(i):
+            nc.scalar.activation(out=t_of[i][:], in_=t_of[i][:], func=ACT.Ln, bias=ln_floor[:])
+
+        def mish_tanh(i):
+            nc.scalar.activation(out=t_of[i][:], in_=t_of[i][:], func=ACT.Tanh, scale=-1.0)
+            h = rows.tile([P, D_HID], BF16)
+            nc.gpsimd.tensor_tensor(out=h[:], in0=y_of[i][:], in1=t_of[i][:], op=ALU.mult)
+            h_of[i] = h
+
+        def quantise_hidden(i):
+            words = h_of[i][:].bitcast(F32)
+            h_t = psum.tile([P, HID_PASSES, 2, P], F32, tag="bank")
+            for g in range(HID_PASSES):
+                for half in range(2):
+                    nc.tensor.transpose(
+                        h_t[:, g, half, :],
+                        words[:, g * K_PASS // 2 + half : (g + 1) * K_PASS // 2 : 2],
+                        ident[:],
+                    )
+            h_grouped = work.tile([P, HID_PASSES * P * PACK], BF16, align_bytes=64)
+            nc.vector.tensor_copy(
+                out=h_grouped[:].bitcast(F32).rearrange("p (g b h) -> p g b h", g=HID_PASSES, h=2),
+                in_=h_t[:].rearrange("p g h b -> p g b h"),
+            )
+            h_codes = work.tile([P, HID_PASSES * P], U32, align_bytes=64)
+            h_scales = work.tile([P, HID_PASSES * P], U8, align_bytes=64)
+            nc.vector.quantize_mx(out=h_codes[:].bitcast(FP8X4), scales=h_scales[:], in_=h_grouped[:])
+            codes_of[i] = (h_codes, h_scales)
+
+        def second_layer(i):
+            h_codes, h_scales = codes_of[i]
+            for j in range(D_OUT // BANK):
+                cols = slice(j * BANK, (j + 1) * BANK)
+                acc = psum.tile([P, BANK], F32, tag="bank")
+                for g in range(HID_PASSES):
+                    batch = slice(g * P, (g + 1) * P)
+                    nc.tensor.matmul_mx(
+                        out=acc[:],
+                        lhsT=h_codes[:, batch].bitcast(FP8X4),
+                        lhsT_scale=h_scales[:, batch],
+                        rhs=w3_words[:, g, cols].bitcast(FP8X4),
+                        rhs_scale=planes[PACK * g : P, cols],
+                        start=(g == 0),
+                        stop=(g == HID_PASSES - 1),
+                    )
+                logit = result.tile([P, BANK], F32)
+                nc.vector.tensor_tensor(
+                    out=logit[:],
+                    in0=acc[:],
+                    in1=spread[:, OUT_BIAS + j * BANK : OUT_BIAS + (j + 1) * BANK],
+                    op=ALU.add,
+                )
+                prob = result.tile([P, BANK], F32)
+                nc.scalar.activation(out=prob[:], in_=logit[:], func=ACT.Sigmoid)
+                nc.sync.dma_start(out=out[i * P : (i + 1) * P, cols], in_=prob[:])
+
+        transpose_x(0)
+        quantise_x(0)
+        spread_vectors(GAIN, 2 * D_HID)
+        first_matmul(0)
+        first_matmul(1)
+        for c in range(1, TILES // 2):
+            transpose_x(c)
+        spread_vectors(OUT_BIAS, D_OUT)
+        round_a = range(0, ROUND)
+        round_b = range(ROUND, TILES)
+        for i in round_a:
+            first_layer(i)
+            mish_sigmoid(i)
+        for i in round_a:
+            mish_ln(i)
+        for i in round_b:
+            first_layer(i)
+        for i in round_a:
+            mish_tanh(i)
+        for i in round_b:
+            mish_sigmoid(i)
+        for i in round_b:
+            mish_ln(i)
+        for i in round_b:
+            mish_tanh(i)
+        quantise_hidden(0)
+        for i in range(TILES):
+            if i + 1 < TILES:
+                quantise_hidden(i + 1)
+            second_layer(i)

@@ -36,7 +36,8 @@ def tile_autoencoder_pb_kernel(tc, h_dec1, D2_words, D2_scales, g4, b4, D3_words
         small = stack.enter_context(tc.tile_pool(name="small", bufs=4))
         rows = stack.enter_context(tc.tile_pool(name="rows", bufs=TILES))
         work = stack.enter_context(tc.tile_pool(name="work", bufs=2))
-        result = stack.enter_context(tc.tile_pool(name="result", bufs=4))
+        logits = stack.enter_context(tc.tile_pool(name="logits", bufs=4))
+        probs = stack.enter_context(tc.tile_pool(name="probs", bufs=12))
         psum = stack.enter_context(tc.psum_pool(name="psum", bufs=8))
 
         planes = keep.tile([P, D_OUT], U8, align_bytes=64)
@@ -117,6 +118,7 @@ def tile_autoencoder_pb_kernel(tc, h_dec1, D2_words, D2_scales, g4, b4, D3_words
             nc.vector.quantize_mx(out=x_codes[:, cols].bitcast(FP8X4), scales=x_scales[:, cols], in_=x_pair(c))
 
         u_of = {}
+        stats_of = {}
         y_of = {}
         t_of = {}
         h_of = {}
@@ -139,7 +141,7 @@ def tile_autoencoder_pb_kernel(tc, h_dec1, D2_words, D2_scales, g4, b4, D3_words
                 )
                 u_of[i].append(u)
 
-        def layer_norm(i):
+        def statistics(i):
             stats = small.tile([P, HID_BANKS, 6], F32)
             for j in range(HID_BANKS):
                 nc.vector.bn_stats(out=stats[:, j, :], in_=u_of[i][j][:])
@@ -151,6 +153,10 @@ def tile_autoencoder_pb_kernel(tc, h_dec1, D2_words, D2_scales, g4, b4, D3_words
             )
             rstd = small.tile([P, 1], F32)
             nc.gpsimd.tensor_tensor(out=rstd[:], in0=var_eps[:], in1=minus_half[:], op=ALU.pow)
+            stats_of[i] = (mean_var, rstd)
+
+        def normalise(i):
+            mean_var, rstd = stats_of[i]
             centred = work.tile([P, D_HID], F32)
             for j in range(HID_BANKS):
                 cols = slice(j * BANK, (j + 1) * BANK)
@@ -174,11 +180,13 @@ def tile_autoencoder_pb_kernel(tc, h_dec1, D2_words, D2_scales, g4, b4, D3_words
             y_of[i] = y
 
         def first_layer(i):
-            layer_norm(i)
+            if i + 1 < TILES:
+                statistics(i + 1)
             if i + 2 < TILES:
                 if i % 2 == 0:
                     quantise_x(i // 2 + 1)
                 first_matmul(i + 2)
+            normalise(i)
 
         def mish_sigmoid(i):
             t = rows.tile([P, D_HID], F32)
@@ -230,14 +238,14 @@ def tile_autoencoder_pb_kernel(tc, h_dec1, D2_words, D2_scales, g4, b4, D3_words
                         start=(g == 0),
                         stop=(g == HID_PASSES - 1),
                     )
-                logit = result.tile([P, BANK], F32)
+                logit = logits.tile([P, BANK], F32)
                 nc.vector.tensor_tensor(
                     out=logit[:],
                     in0=acc[:],
                     in1=spread[:, OUT_BIAS + j * BANK : OUT_BIAS + (j + 1) * BANK],
                     op=ALU.add,
                 )
-                prob = result.tile([P, BANK], F32)
+                prob = probs.tile([P, BANK], F32)
                 nc.scalar.activation(out=prob[:], in_=logit[:], func=ACT.Sigmoid)
                 nc.sync.dma_start(out=out[i * P : (i + 1) * P, cols], in_=prob[:])
 
@@ -249,23 +257,24 @@ def tile_autoencoder_pb_kernel(tc, h_dec1, D2_words, D2_scales, g4, b4, D3_words
         for c in range(1, TILES // 2):
             transpose_x(c)
         spread_vectors(OUT_BIAS, D_OUT)
-        round_a = range(0, ROUND)
-        round_b = range(ROUND, TILES)
-        for i in round_a:
+        statistics(0)
+        short = TILES % ROUND
+        starts = [0] + list(range(short if short else ROUND, TILES, ROUND))
+        rounds = [range(a, b) for a, b in zip(starts, starts[1:] + [TILES])]
+        for i in rounds[0]:
             first_layer(i)
             mish_sigmoid(i)
-        for i in round_a:
-            mish_ln(i)
-        for i in round_b:
-            first_layer(i)
-        for i in round_a:
-            mish_tanh(i)
-        for i in round_b:
-            mish_sigmoid(i)
-        for i in round_b:
-            mish_ln(i)
-        for i in round_b:
-            mish_tanh(i)
+        for r in range(len(rounds)):
+            for i in rounds[r]:
+                mish_ln(i)
+            if r + 1 < len(rounds):
+                for i in rounds[r + 1]:
+                    first_layer(i)
+            for i in rounds[r]:
+                mish_tanh(i)
+            if r + 1 < len(rounds):
+                for i in rounds[r + 1]:
+                    mish_sigmoid(i)
         quantise_hidden(0)
         for i in range(TILES):
             if i + 1 < TILES:

@@ -36,15 +36,14 @@ def tile_autoencoder_pb_kernel(tc, h_dec1, D2_words, D2_scales, g4, b4, D3_words
         small = stack.enter_context(tc.tile_pool(name="small", bufs=4))
         rows = stack.enter_context(tc.tile_pool(name="rows", bufs=TILES))
         work = stack.enter_context(tc.tile_pool(name="work", bufs=2))
-        logits = stack.enter_context(tc.tile_pool(name="logits", bufs=4))
-        probs = stack.enter_context(tc.tile_pool(name="probs", bufs=12))
-        psum = stack.enter_context(tc.psum_pool(name="psum", bufs=8))
+        psum_mx = stack.enter_context(tc.psum_pool(name="psum_mx", bufs=6))
+        psum_tr = stack.enter_context(tc.psum_pool(name="psum_tr", bufs=2))
 
         planes = keep.tile([P, D_OUT], U8, align_bytes=64)
         nc.vector.memset(planes[:].bitcast(I32), 0)
         D2_PLANE = 2 * PACK
-        GAIN, SHIFT, OUT_BIAS = 0, D_HID, 2 * D_HID
-        vectors = keep.tile([P, 2 * D_HID + D_OUT], BF16)
+        GAIN, SHIFT = 0, D_HID
+        vectors = keep.tile([P, 2 * D_HID], BF16)
         nc.vector.memset(vectors[:], 0.0)
         ones = keep.tile([P, P], BF16)
         nc.vector.memset(ones[:], 1.0)
@@ -72,7 +71,6 @@ def tile_autoencoder_pb_kernel(tc, h_dec1, D2_words, D2_scales, g4, b4, D3_words
         )
         nc.scalar.dma_start(out=vectors[0:1, GAIN : GAIN + D_HID], in_=g4.unsqueeze(0))
         nc.scalar.dma_start(out=vectors[0:1, SHIFT : SHIFT + D_HID], in_=b4.unsqueeze(0))
-        nc.scalar.dma_start(out=vectors[0:1, OUT_BIAS : OUT_BIAS + D_OUT], in_=bo.unsqueeze(0))
         nc.sync.dma_start(out=x_sb[:, 2:TILES, :], in_=x_rows[:, 2:TILES, :])
         for quad in range(4):
             nc.sync.dma_start(
@@ -85,11 +83,13 @@ def tile_autoencoder_pb_kernel(tc, h_dec1, D2_words, D2_scales, g4, b4, D3_words
                 in_=D3_words[g].rearrange("p n t -> p (n t)").bitcast(I32),
             )
 
-        spread = keep.tile([P, 2 * D_HID + D_OUT], BF16)
+        out_bias = keep.tile([P, D_OUT], BF16)
+        nc.sync.dma_start(out=out_bias[:], in_=bo.partition_broadcast(P))
+        spread = keep.tile([P, 2 * D_HID], BF16)
 
-        def spread_vectors(first_col, width):
-            for col in range(first_col, first_col + width, BANK):
-                summed = psum.tile([P, BANK], F32, tag="bank")
+        def spread_vectors():
+            for col in range(0, 2 * D_HID, BANK):
+                summed = psum_tr.tile([P, BANK], F32, tag="tr")
                 nc.tensor.matmul(
                     out=summed[:], lhsT=ones[:], rhs=vectors[:, col : col + BANK], start=True, stop=True
                 )
@@ -103,7 +103,7 @@ def tile_autoencoder_pb_kernel(tc, h_dec1, D2_words, D2_scales, g4, b4, D3_words
             return x_grouped[:, 2 * c : 2 * c + 2, :, :].rearrange("p i b t -> p (i b t)")
 
         def transpose_x(c):
-            x_t = psum.tile([P, 2, 2, P], F32, tag="bank")
+            x_t = psum_tr.tile([P, 2, 2, P], F32, tag="tr")
             for i in range(2):
                 words = x_sb[:, 2 * c + i, :].bitcast(F32)
                 for half in range(2):
@@ -129,7 +129,7 @@ def tile_autoencoder_pb_kernel(tc, h_dec1, D2_words, D2_scales, g4, b4, D3_words
             u_of[i] = []
             for j in range(HID_BANKS):
                 cols = slice(j * BANK, (j + 1) * BANK)
-                u = psum.tile([P, BANK], F32, tag="bank")
+                u = psum_mx.tile([P, BANK], F32, tag="mx")
                 nc.tensor.matmul_mx(
                     out=u[:],
                     lhsT=x_codes[:, batch].bitcast(FP8X4),
@@ -182,9 +182,11 @@ def tile_autoencoder_pb_kernel(tc, h_dec1, D2_words, D2_scales, g4, b4, D3_words
         def first_layer(i):
             if i + 1 < TILES:
                 statistics(i + 1)
+            if i % 2 == 0 and i + 2 < TILES:
+                quantise_x(i // 2 + 1)
+            if i % 2 == 0 and i + 4 < TILES:
+                transpose_x(i // 2 + 2)
             if i + 2 < TILES:
-                if i % 2 == 0:
-                    quantise_x(i // 2 + 1)
                 first_matmul(i + 2)
             normalise(i)
 
@@ -204,7 +206,7 @@ def tile_autoencoder_pb_kernel(tc, h_dec1, D2_words, D2_scales, g4, b4, D3_words
 
         def quantise_hidden(i):
             words = h_of[i][:].bitcast(F32)
-            h_t = psum.tile([P, HID_PASSES, 2, P], F32, tag="bank")
+            h_t = psum_tr.tile([P, HID_PASSES, 2, P], F32, tag="tr")
             for g in range(HID_PASSES):
                 for half in range(2):
                     nc.tensor.transpose(
@@ -222,11 +224,13 @@ def tile_autoencoder_pb_kernel(tc, h_dec1, D2_words, D2_scales, g4, b4, D3_words
             nc.vector.quantize_mx(out=h_codes[:].bitcast(FP8X4), scales=h_scales[:], in_=h_grouped[:])
             codes_of[i] = (h_codes, h_scales)
 
+        out_sb = keep.tile([P, TILES, D_OUT], F32)
+
         def second_layer(i):
             h_codes, h_scales = codes_of[i]
             for j in range(D_OUT // BANK):
                 cols = slice(j * BANK, (j + 1) * BANK)
-                acc = psum.tile([P, BANK], F32, tag="bank")
+                acc = psum_mx.tile([P, BANK], F32, tag="mx")
                 for g in range(HID_PASSES):
                     batch = slice(g * P, (g + 1) * P)
                     nc.tensor.matmul_mx(
@@ -238,25 +242,21 @@ def tile_autoencoder_pb_kernel(tc, h_dec1, D2_words, D2_scales, g4, b4, D3_words
                         start=(g == 0),
                         stop=(g == HID_PASSES - 1),
                     )
-                logit = logits.tile([P, BANK], F32)
                 nc.vector.tensor_tensor(
-                    out=logit[:],
+                    out=out_sb[:, i, cols],
                     in0=acc[:],
-                    in1=spread[:, OUT_BIAS + j * BANK : OUT_BIAS + (j + 1) * BANK],
+                    in1=out_bias[:, cols],
                     op=ALU.add,
                 )
-                prob = probs.tile([P, BANK], F32)
-                nc.scalar.activation(out=prob[:], in_=logit[:], func=ACT.Sigmoid)
-                nc.sync.dma_start(out=out[i * P : (i + 1) * P, cols], in_=prob[:])
+                nc.scalar.activation(out=out_sb[:, i, cols], in_=out_sb[:, i, cols], func=ACT.Sigmoid)
+                nc.sync.dma_start(out=out[i * P : (i + 1) * P, cols], in_=out_sb[:, i, cols])
 
         transpose_x(0)
         quantise_x(0)
-        spread_vectors(GAIN, 2 * D_HID)
         first_matmul(0)
         first_matmul(1)
-        for c in range(1, TILES // 2):
-            transpose_x(c)
-        spread_vectors(OUT_BIAS, D_OUT)
+        transpose_x(1)
+        spread_vectors()
         statistics(0)
         short = TILES % ROUND
         starts = [0] + list(range(short if short else ROUND, TILES, ROUND))

@@ -21,7 +21,7 @@ BATCH, D_IN, D_HID, D_OUT = 1024, 512, 1024, 1536
 TILES = BATCH // P
 HID_BANKS = D_HID // BANK
 HID_PASSES = D_HID // K_PASS
-ROUND = 4
+BLOCKS = D_HID // P
 EPS = 1e-5
 LN_FLOOR = 2.0**-60
 
@@ -33,20 +33,16 @@ def tile_autoencoder_pb_kernel(tc, h_dec1, D2_words, D2_scales, g4, b4, D3_words
     with ExitStack() as stack:
         stack.enter_context(tc.manual_schedule())
         keep = stack.enter_context(tc.tile_pool(name="keep", bufs=1))
-        small = stack.enter_context(tc.tile_pool(name="small", bufs=4))
+        small = stack.enter_context(tc.tile_pool(name="small", bufs=TILES))
         rows = stack.enter_context(tc.tile_pool(name="rows", bufs=TILES))
-        work = stack.enter_context(tc.tile_pool(name="work", bufs=2))
+        pairs = stack.enter_context(tc.tile_pool(name="pairs", bufs=TILES // 2))
+        work = stack.enter_context(tc.tile_pool(name="work", bufs=4))
         psum_mx = stack.enter_context(tc.psum_pool(name="psum_mx", bufs=6))
         psum_tr = stack.enter_context(tc.psum_pool(name="psum_tr", bufs=2))
 
         planes = keep.tile([P, D_OUT], U8, align_bytes=64)
         nc.vector.memset(planes[:].bitcast(I32), 0)
         D2_PLANE = 2 * PACK
-        GAIN, SHIFT = 0, D_HID
-        vectors = keep.tile([P, 2 * D_HID], BF16)
-        nc.vector.memset(vectors[:], 0.0)
-        ones = keep.tile([P, P], BF16)
-        nc.vector.memset(ones[:], 1.0)
         ln_floor = keep.tile([P, 1], F32)
         nc.vector.memset(ln_floor[:], LN_FLOOR)
         minus_half = keep.tile([P, 1], F32)
@@ -69,9 +65,15 @@ def tile_autoencoder_pb_kernel(tc, h_dec1, D2_words, D2_scales, g4, b4, D3_words
         nc.sync.dma_start(
             out=w2_words[:].bitcast(I32), in_=D2_words[0].rearrange("p n t -> p (n t)").bitcast(I32)
         )
-        nc.scalar.dma_start(out=vectors[0:1, GAIN : GAIN + D_HID], in_=g4.unsqueeze(0))
-        nc.scalar.dma_start(out=vectors[0:1, SHIFT : SHIFT + D_HID], in_=b4.unsqueeze(0))
-        nc.sync.dma_start(out=x_sb[:, 2:TILES, :], in_=x_rows[:, 2:TILES, :])
+        nc.sync.dma_start(out=x_sb[:, 2:4, :], in_=x_rows[:, 2:4, :])
+        gain_bf = keep.tile([P, BLOCKS], BF16)
+        shift_bf = keep.tile([P, BLOCKS], BF16)
+        for column, vector in ((gain_bf, g4), (shift_bf, b4)):
+            nc.scalar.dma_start(
+                out=column[:].rearrange("p (g t) -> p g t", t=PACK),
+                in_=vector.rearrange("(g p t) -> p g t", p=P, t=PACK),
+            )
+        nc.sync.dma_start(out=x_sb[:, 4:TILES, :], in_=x_rows[:, 4:TILES, :])
         for quad in range(4):
             nc.sync.dma_start(
                 out=planes[32 * quad : 32 * quad + 4 * HID_PASSES, :].bitcast(I32),
@@ -82,18 +84,20 @@ def tile_autoencoder_pb_kernel(tc, h_dec1, D2_words, D2_scales, g4, b4, D3_words
                 out=w3_words[:, g, :].bitcast(I32),
                 in_=D3_words[g].rearrange("p n t -> p (n t)").bitcast(I32),
             )
-
         out_bias = keep.tile([P, D_OUT], BF16)
         nc.sync.dma_start(out=out_bias[:], in_=bo.partition_broadcast(P))
-        spread = keep.tile([P, 2 * D_HID], BF16)
 
-        def spread_vectors():
-            for col in range(0, 2 * D_HID, BANK):
-                summed = psum_tr.tile([P, BANK], F32, tag="tr")
-                nc.tensor.matmul(
-                    out=summed[:], lhsT=ones[:], rhs=vectors[:, col : col + BANK], start=True, stop=True
+        gain = keep.tile([P, BLOCKS], F32)
+        shift = keep.tile([P, BLOCKS], F32)
+        minus_gain = keep.tile([P, BLOCKS], F32)
+        minus_shift = keep.tile([P, BLOCKS], F32)
+
+        def columns():
+            for plain, minus, column in ((gain, minus_gain, gain_bf), (shift, minus_shift, shift_bf)):
+                nc.vector.tensor_copy(out=plain[:], in_=column[:])
+                nc.vector.tensor_scalar(
+                    out=minus[:], in0=column[:], scalar1=-1.0, scalar2=None, op0=ALU.mult
                 )
-                nc.scalar.copy(out=spread[:, col : col + BANK], in_=summed[:])
 
         x_grouped = keep.tile([P, TILES, P, PACK], BF16, align_bytes=64)
         x_codes = keep.tile([P, TILES * P], U32, align_bytes=64)
@@ -119,9 +123,9 @@ def tile_autoencoder_pb_kernel(tc, h_dec1, D2_words, D2_scales, g4, b4, D3_words
 
         u_of = {}
         stats_of = {}
+        z_of = {}
         y_of = {}
         t_of = {}
-        h_of = {}
         codes_of = {}
 
         def first_matmul(i):
@@ -141,7 +145,7 @@ def tile_autoencoder_pb_kernel(tc, h_dec1, D2_words, D2_scales, g4, b4, D3_words
                 )
                 u_of[i].append(u)
 
-        def statistics(i):
+        def statistics(i, offset_too):
             stats = small.tile([P, HID_BANKS, 6], F32)
             for j in range(HID_BANKS):
                 nc.vector.bn_stats(out=stats[:, j, :], in_=u_of[i][j][:])
@@ -153,101 +157,128 @@ def tile_autoencoder_pb_kernel(tc, h_dec1, D2_words, D2_scales, g4, b4, D3_words
             )
             rstd = small.tile([P, 1], F32)
             nc.gpsimd.tensor_tensor(out=rstd[:], in0=var_eps[:], in1=minus_half[:], op=ALU.pow)
-            stats_of[i] = (mean_var, rstd)
+            offset = None
+            if offset_too:
+                minus_mean = small.tile([P, 1], F32)
+                nc.gpsimd.tensor_scalar(
+                    out=minus_mean[:], in0=mean_var[:, 0:1], scalar1=-1.0, scalar2=0.0, op0=ALU.mult, op1=ALU.add
+                )
+                offset = small.tile([P, 1], F32)
+                nc.gpsimd.tensor_tensor(out=offset[:], in0=minus_mean[:], in1=rstd[:], op=ALU.mult)
+            stats_of[i] = (mean_var, rstd, offset)
+
+        def z_views(i, j):
+            return (
+                z_of[i][:, j * BANK : (j + 1) * BANK].rearrange("p (t q) -> p t q", t=PACK),
+                u_of[i][j][:].rearrange("p (q t) -> p t q", t=PACK),
+            )
 
         def normalise(i):
-            mean_var, rstd = stats_of[i]
-            centred = work.tile([P, D_HID], F32)
+            mean_var, rstd, offset = stats_of[i]
+            z_of[i] = rows.tile([P, D_HID], F32, name="z")
             for j in range(HID_BANKS):
-                cols = slice(j * BANK, (j + 1) * BANK)
-                nc.vector.scalar_tensor_tensor(
-                    out=centred[:, cols],
-                    in0=u_of[i][j][:],
-                    scalar=mean_var[:, 0:1],
-                    in1=spread[:, GAIN + j * BANK : GAIN + (j + 1) * BANK],
-                    op0=ALU.subtract,
-                    op1=ALU.mult,
-                )
-            y = rows.tile([P, D_HID], F32)
-            nc.vector.scalar_tensor_tensor(
-                out=y[:],
-                in0=centred[:],
-                scalar=rstd[:],
-                in1=spread[:, SHIFT : SHIFT + D_HID],
-                op0=ALU.mult,
-                op1=ALU.add,
-            )
-            y_of[i] = y
-
-        def first_layer(i):
-            if i + 1 < TILES:
-                statistics(i + 1)
-            if i % 2 == 0 and i + 2 < TILES:
-                quantise_x(i // 2 + 1)
-            if i % 2 == 0 and i + 4 < TILES:
-                transpose_x(i // 2 + 2)
-            if i + 2 < TILES:
-                first_matmul(i + 2)
-            normalise(i)
-
-        def mish_sigmoid(i):
-            t = rows.tile([P, D_HID], F32)
-            nc.scalar.activation(out=t[:], in_=y_of[i][:], func=ACT.Sigmoid, scale=-1.0)
-            t_of[i] = t
-
-        def mish_ln(i):
-            nc.scalar.activation(out=t_of[i][:], in_=t_of[i][:], func=ACT.Ln, bias=ln_floor[:])
-
-        def mish_tanh(i):
-            nc.scalar.activation(out=t_of[i][:], in_=t_of[i][:], func=ACT.Tanh, scale=-1.0)
-            h = rows.tile([P, D_HID], BF16)
-            nc.gpsimd.tensor_tensor(out=h[:], in0=y_of[i][:], in1=t_of[i][:], op=ALU.mult)
-            h_of[i] = h
-
-        def quantise_hidden(i):
-            words = h_of[i][:].bitcast(F32)
-            h_t = psum_tr.tile([P, HID_PASSES, 2, P], F32, tag="tr")
-            for g in range(HID_PASSES):
-                for half in range(2):
-                    nc.tensor.transpose(
-                        h_t[:, g, half, :],
-                        words[:, g * K_PASS // 2 + half : (g + 1) * K_PASS // 2 : 2],
-                        ident[:],
+                z, u = z_views(i, j)
+                if offset is None:
+                    nc.vector.tensor_scalar(
+                        out=z, in0=u, scalar1=mean_var[:, 0:1], scalar2=rstd[:], op0=ALU.subtract, op1=ALU.mult
                     )
-            h_grouped = work.tile([P, HID_PASSES * P * PACK], BF16, align_bytes=64)
-            nc.vector.tensor_copy(
-                out=h_grouped[:].bitcast(F32).rearrange("p (g b h) -> p g b h", g=HID_PASSES, h=2),
-                in_=h_t[:].rearrange("p g h b -> p g b h"),
-            )
-            h_codes = work.tile([P, HID_PASSES * P], U32, align_bytes=64)
-            h_scales = work.tile([P, HID_PASSES * P], U8, align_bytes=64)
-            nc.vector.quantize_mx(out=h_codes[:].bitcast(FP8X4), scales=h_scales[:], in_=h_grouped[:])
-            codes_of[i] = (h_codes, h_scales)
+                else:
+                    nc.scalar.activation(out=z, in_=u, func=ACT.Identity, scale=rstd[:], bias=offset[:])
+
+        def turn(c, bank):
+            z_t = psum_tr.tile([P, 2, 2 * P], F32, tag="tr")
+            for b in range(2):
+                for i in range(2):
+                    cols = slice((2 * bank + b) * P, (2 * bank + b + 1) * P)
+                    nc.tensor.transpose(z_t[:, b, i * P : (i + 1) * P], z_of[2 * c + i][:, cols], ident[:])
+            return z_t
+
+        def mish_sigmoid(c, bank):
+            if bank == 0:
+                t_of[c] = pairs.tile([P, BLOCKS, 2 * P], F32, name="t")
+            z_t = turn(c, bank)
+            for b in range(2):
+                block = 2 * bank + b
+                nc.scalar.activation(
+                    out=t_of[c][:, block, :],
+                    in_=z_t[:, b, :],
+                    func=ACT.Sigmoid,
+                    scale=minus_gain[:, block : block + 1],
+                    bias=minus_shift[:, block : block + 1],
+                )
+
+        def affine(c):
+            y = pairs.tile([P, BLOCKS, 2 * P], F32, name="y")
+            for bank in range(BLOCKS // 2):
+                z_t = turn(c, bank)
+                for b in range(2):
+                    block = 2 * bank + b
+                    nc.vector.tensor_scalar(
+                        out=y[:, block, :],
+                        in0=z_t[:, b, :],
+                        scalar1=gain[:, block : block + 1],
+                        scalar2=shift[:, block : block + 1],
+                        op0=ALU.mult,
+                        op1=ALU.add,
+                    )
+            y_of[c] = y
+
+        def mish_ln(c):
+            nc.scalar.activation(out=t_of[c][:], in_=t_of[c][:], func=ACT.Ln, bias=ln_floor[:])
+
+        def mish_tanh(c):
+            for g in range(HID_PASSES):
+                blocks = slice(PACK * g, PACK * (g + 1))
+                nc.scalar.activation(out=t_of[c][:, blocks, :], in_=t_of[c][:, blocks, :], func=ACT.Tanh, scale=-1.0)
+
+        def multiply_hidden(c, engine):
+            grouped = []
+            for g in range(HID_PASSES):
+                blocks = slice(PACK * g, PACK * (g + 1))
+                h = work.tile([P, 2 * P, PACK], BF16, align_bytes=64, name="h")
+                engine.tensor_tensor(
+                    out=h[:],
+                    in0=y_of[c][:, blocks, :].rearrange("p t b -> p b t"),
+                    in1=t_of[c][:, blocks, :].rearrange("p t b -> p b t"),
+                    op=ALU.mult,
+                )
+                grouped.append(h)
+            codes_of[c] = grouped
+
+        def quantise_hidden(c):
+            grouped = codes_of[c]
+            codes_of[c] = []
+            for h in grouped:
+                codes = work.tile([P, 2 * P], U32, align_bytes=64, name="codes")
+                scales = work.tile([P, 2 * P], U8, align_bytes=64, name="scales")
+                nc.vector.quantize_mx(
+                    out=codes[:].bitcast(FP8X4), scales=scales[:], in_=h[:].rearrange("p b t -> p (b t)")
+                )
+                codes_of[c].append((codes, scales))
 
         out_sb = keep.tile([P, TILES, D_OUT], F32)
 
-        def second_layer(i):
-            h_codes, h_scales = codes_of[i]
+        def second_matmul(i):
+            batch = slice((i % 2) * P, (i % 2 + 1) * P)
             for j in range(D_OUT // BANK):
                 cols = slice(j * BANK, (j + 1) * BANK)
                 acc = psum_mx.tile([P, BANK], F32, tag="mx")
                 for g in range(HID_PASSES):
-                    batch = slice(g * P, (g + 1) * P)
+                    codes, scales = codes_of[i // 2][g]
                     nc.tensor.matmul_mx(
                         out=acc[:],
-                        lhsT=h_codes[:, batch].bitcast(FP8X4),
-                        lhsT_scale=h_scales[:, batch],
+                        lhsT=codes[:, batch].bitcast(FP8X4),
+                        lhsT_scale=scales[:, batch],
                         rhs=w3_words[:, g, cols].bitcast(FP8X4),
                         rhs_scale=planes[PACK * g : P, cols],
                         start=(g == 0),
                         stop=(g == HID_PASSES - 1),
                     )
-                nc.vector.tensor_tensor(
-                    out=out_sb[:, i, cols],
-                    in0=acc[:],
-                    in1=out_bias[:, cols],
-                    op=ALU.add,
-                )
+                nc.vector.tensor_tensor(out=out_sb[:, i, cols], in0=acc[:], in1=out_bias[:, cols], op=ALU.add)
+
+        def finish(i):
+            for j in range(D_OUT // BANK):
+                cols = slice(j * BANK, (j + 1) * BANK)
                 nc.scalar.activation(out=out_sb[:, i, cols], in_=out_sb[:, i, cols], func=ACT.Sigmoid)
                 nc.sync.dma_start(out=out[i * P : (i + 1) * P, cols], in_=out_sb[:, i, cols])
 
@@ -256,27 +287,74 @@ def tile_autoencoder_pb_kernel(tc, h_dec1, D2_words, D2_scales, g4, b4, D3_words
         first_matmul(0)
         first_matmul(1)
         transpose_x(1)
-        spread_vectors()
-        statistics(0)
-        short = TILES % ROUND
-        starts = [0] + list(range(short if short else ROUND, TILES, ROUND))
-        rounds = [range(a, b) for a, b in zip(starts, starts[1:] + [TILES])]
-        for i in rounds[0]:
-            first_layer(i)
-            mish_sigmoid(i)
-        for r in range(len(rounds)):
-            for i in rounds[r]:
-                mish_ln(i)
-            if r + 1 < len(rounds):
-                for i in rounds[r + 1]:
-                    first_layer(i)
-            for i in rounds[r]:
-                mish_tanh(i)
-            if r + 1 < len(rounds):
-                for i in rounds[r + 1]:
-                    mish_sigmoid(i)
+        transpose_x(2)
+        statistics(0, True)
+        quantise_x(1)
+        first_matmul(2)
+        transpose_x(3)
+        statistics(1, False)
+        columns()
+        normalise(0)
+        statistics(2, True)
+        quantise_x(2)
+        first_matmul(3)
+        normalise(1)
+        normalise(2)
+        mish_sigmoid(0, 0)
+        mish_sigmoid(0, 1)
+        first_matmul(4)
+        statistics(3, False)
+        mish_sigmoid(0, 2)
+        statistics(4, True)
+        first_matmul(5)
+        mish_sigmoid(0, 3)
+        normalise(3)
+        normalise(4)
+        quantise_x(3)
+        statistics(5, False)
+        mish_sigmoid(1, 0)
+        mish_sigmoid(1, 1)
+        first_matmul(6)
+        statistics(6, True)
+        mish_sigmoid(1, 2)
+        first_matmul(7)
+        mish_sigmoid(1, 3)
+        normalise(5)
+        normalise(6)
+        statistics(7, False)
+        for bank in range(BLOCKS // 2):
+            mish_sigmoid(2, bank)
+        normalise(7)
+        for bank in range(BLOCKS // 2):
+            mish_sigmoid(3, bank)
+        for c in range(TILES // 2):
+            mish_ln(c)
+            affine(c)
+        mish_tanh(0)
+        multiply_hidden(0, nc.vector)
         quantise_hidden(0)
-        for i in range(TILES):
-            if i + 1 < TILES:
-                quantise_hidden(i + 1)
-            second_layer(i)
+        mish_tanh(1)
+        multiply_hidden(1, nc.gpsimd)
+        mish_tanh(2)
+        multiply_hidden(2, nc.gpsimd)
+        second_matmul(0)
+        second_matmul(1)
+        finish(0)
+        finish(1)
+        mish_tanh(3)
+        quantise_hidden(1)
+        second_matmul(2)
+        multiply_hidden(3, nc.vector)
+        quantise_hidden(3)
+        second_matmul(3)
+        finish(2)
+        finish(3)
+        second_matmul(6)
+        second_matmul(7)
+        finish(6)
+        finish(7)
+        quantise_hidden(2)
+        second_matmul(4)
+        second_matmul(5)
+        finish(4)
+        finish(5)

@@ -22,6 +22,8 @@ TILES = BATCH // P
 HID_BANKS = D_HID // BANK
 HID_PASSES = D_HID // K_PASS
 BLOCKS = D_HID // P
+RUN = 4
+RUNS = 2 * P // RUN
 EPS = 1e-5
 LN_FLOOR = 2.0**-60
 
@@ -40,9 +42,10 @@ def tile_autoencoder_pb_kernel(tc, h_dec1, D2_words, D2_scales, g4, b4, D3_words
         psum_mx = stack.enter_context(tc.psum_pool(name="psum_mx", bufs=6))
         psum_tr = stack.enter_context(tc.psum_pool(name="psum_tr", bufs=2))
 
+        d2_plane = keep.tile([P, D_HID], U8, align_bytes=64)
+        nc.vector.memset(d2_plane[:].bitcast(I32), 0)
         planes = keep.tile([P, D_OUT], U8, align_bytes=64)
         nc.vector.memset(planes[:].bitcast(I32), 0)
-        D2_PLANE = 2 * PACK
         ln_floor = keep.tile([P, 1], F32)
         nc.vector.memset(ln_floor[:], LN_FLOOR)
         minus_half = keep.tile([P, 1], F32)
@@ -59,7 +62,7 @@ def tile_autoencoder_pb_kernel(tc, h_dec1, D2_words, D2_scales, g4, b4, D3_words
         nc.sync.dma_start(out=x_sb[:, 0:2, :], in_=x_rows[:, 0:2, :])
         for quad in range(4):
             nc.sync.dma_start(
-                out=planes[32 * quad + D2_PLANE : 32 * quad + D2_PLANE + 4, 0:D_HID].bitcast(I32),
+                out=d2_plane[32 * quad : 32 * quad + 4, :].bitcast(I32),
                 in_=D2_scales[0, 4 * quad : 4 * quad + 4, :].bitcast(I32),
             )
         nc.sync.dma_start(
@@ -123,10 +126,12 @@ def tile_autoencoder_pb_kernel(tc, h_dec1, D2_words, D2_scales, g4, b4, D3_words
 
         u_of = {}
         stats_of = {}
+        offset_of = {}
         z_of = {}
         y_of = {}
         t_of = {}
         codes_of = {}
+        acc_of = {}
 
         def first_matmul(i):
             batch = slice(i * P, (i + 1) * P)
@@ -139,13 +144,13 @@ def tile_autoencoder_pb_kernel(tc, h_dec1, D2_words, D2_scales, g4, b4, D3_words
                     lhsT=x_codes[:, batch].bitcast(FP8X4),
                     lhsT_scale=x_scales[:, batch],
                     rhs=w2_words[:, cols].bitcast(FP8X4),
-                    rhs_scale=planes[D2_PLANE:P, cols],
+                    rhs_scale=d2_plane[:, cols],
                     start=True,
                     stop=True,
                 )
                 u_of[i].append(u)
 
-        def statistics(i, offset_too):
+        def statistics(i):
             stats = small.tile([P, HID_BANKS, 6], F32)
             for j in range(HID_BANKS):
                 nc.vector.bn_stats(out=stats[:, j, :], in_=u_of[i][j][:])
@@ -157,15 +162,7 @@ def tile_autoencoder_pb_kernel(tc, h_dec1, D2_words, D2_scales, g4, b4, D3_words
             )
             rstd = small.tile([P, 1], F32)
             nc.gpsimd.tensor_tensor(out=rstd[:], in0=var_eps[:], in1=minus_half[:], op=ALU.pow)
-            offset = None
-            if offset_too:
-                minus_mean = small.tile([P, 1], F32)
-                nc.gpsimd.tensor_scalar(
-                    out=minus_mean[:], in0=mean_var[:, 0:1], scalar1=-1.0, scalar2=0.0, op0=ALU.mult, op1=ALU.add
-                )
-                offset = small.tile([P, 1], F32)
-                nc.gpsimd.tensor_tensor(out=offset[:], in0=minus_mean[:], in1=rstd[:], op=ALU.mult)
-            stats_of[i] = (mean_var, rstd, offset)
+            stats_of[i] = (mean_var, rstd)
 
         def z_views(i, j):
             return (
@@ -173,20 +170,32 @@ def tile_autoencoder_pb_kernel(tc, h_dec1, D2_words, D2_scales, g4, b4, D3_words
                 u_of[i][j][:].rearrange("p (q t) -> p t q", t=PACK),
             )
 
-        def normalise(i):
-            mean_var, rstd, offset = stats_of[i]
+        def offset(i):
+            mean_var, rstd = stats_of[i]
+            offset_of[i] = small.tile([P, 1], F32, name="minus_mean_rstd")
+            nc.vector.scalar_tensor_tensor(
+                out=offset_of[i][:], in0=mean_var[:, 0:1], scalar=-1.0, in1=rstd[:], op0=ALU.mult, op1=ALU.mult
+            )
+
+        def normalise_scalar(i):
             z_of[i] = rows.tile([P, D_HID], F32, name="z")
             for j in range(HID_BANKS):
                 z, u = z_views(i, j)
-                if offset is None:
-                    nc.vector.tensor_scalar(
-                        out=z, in0=u, scalar1=mean_var[:, 0:1], scalar2=rstd[:], op0=ALU.subtract, op1=ALU.mult
-                    )
-                else:
-                    nc.scalar.activation(out=z, in_=u, func=ACT.Identity, scale=rstd[:], bias=offset[:])
+                nc.scalar.activation(
+                    out=z, in_=u, func=ACT.Identity, scale=stats_of[i][1][:], bias=offset_of[i][:]
+                )
 
-        def turn(c, bank):
-            z_t = psum_tr.tile([P, 2, 2 * P], F32, tag="tr")
+        def normalise_vector(i):
+            mean_var, rstd = stats_of[i]
+            z_of[i] = rows.tile([P, D_HID], F32, name="z")
+            for j in range(HID_BANKS):
+                z, u = z_views(i, j)
+                nc.vector.tensor_scalar(
+                    out=z, in0=u, scalar1=mean_var[:, 0:1], scalar2=rstd[:], op0=ALU.subtract, op1=ALU.mult
+                )
+
+        def turn(c, bank, pool, tag):
+            z_t = pool.tile([P, 2, 2 * P], F32, tag=tag, name="z_t")
             for b in range(2):
                 for i in range(2):
                     cols = slice((2 * bank + b) * P, (2 * bank + b + 1) * P)
@@ -195,55 +204,51 @@ def tile_autoencoder_pb_kernel(tc, h_dec1, D2_words, D2_scales, g4, b4, D3_words
 
         def mish_sigmoid(c, bank):
             if bank == 0:
-                t_of[c] = pairs.tile([P, BLOCKS, 2 * P], F32, name="t")
-            z_t = turn(c, bank)
+                t_of[c] = pairs.tile([P, HID_PASSES, RUNS, PACK, RUN], F32, name="t")
+            z_t = turn(c, bank, psum_tr, "tr")
             for b in range(2):
                 block = 2 * bank + b
                 nc.scalar.activation(
-                    out=t_of[c][:, block, :],
-                    in_=z_t[:, b, :],
+                    out=t_of[c][:, block // PACK, :, block % PACK, :],
+                    in_=z_t[:, b, :].rearrange("p (r i) -> p r i", i=RUN),
                     func=ACT.Sigmoid,
                     scale=minus_gain[:, block : block + 1],
                     bias=minus_shift[:, block : block + 1],
                 )
 
-        def affine(c):
-            y = pairs.tile([P, BLOCKS, 2 * P], F32, name="y")
-            for bank in range(BLOCKS // 2):
-                z_t = turn(c, bank)
-                for b in range(2):
-                    block = 2 * bank + b
-                    nc.vector.tensor_scalar(
-                        out=y[:, block, :],
-                        in0=z_t[:, b, :],
-                        scalar1=gain[:, block : block + 1],
-                        scalar2=shift[:, block : block + 1],
-                        op0=ALU.mult,
-                        op1=ALU.add,
-                    )
-            y_of[c] = y
+        def affine(c, bank):
+            if bank == 0:
+                y_of[c] = pairs.tile([P, HID_PASSES, RUNS, PACK, RUN], F32, name="y")
+            z_t = turn(c, bank, psum_mx, "mx")
+            for b in range(2):
+                block = 2 * bank + b
+                nc.vector.tensor_scalar(
+                    out=y_of[c][:, block // PACK, :, block % PACK, :],
+                    in0=z_t[:, b, :].rearrange("p (r i) -> p r i", i=RUN),
+                    scalar1=gain[:, block : block + 1],
+                    scalar2=shift[:, block : block + 1],
+                    op0=ALU.mult,
+                    op1=ALU.add,
+                )
 
         def mish_ln(c):
             nc.scalar.activation(out=t_of[c][:], in_=t_of[c][:], func=ACT.Ln, bias=ln_floor[:])
 
         def mish_tanh(c):
             for g in range(HID_PASSES):
-                blocks = slice(PACK * g, PACK * (g + 1))
-                nc.scalar.activation(out=t_of[c][:, blocks, :], in_=t_of[c][:, blocks, :], func=ACT.Tanh, scale=-1.0)
+                nc.scalar.activation(out=t_of[c][:, g], in_=t_of[c][:, g], func=ACT.Tanh, scale=-1.0)
 
-        def multiply_hidden(c, engine):
-            grouped = []
-            for g in range(HID_PASSES):
-                blocks = slice(PACK * g, PACK * (g + 1))
+        def multiply_hidden(c, engines):
+            codes_of[c] = []
+            for g, engine in enumerate(engines):
                 h = work.tile([P, 2 * P, PACK], BF16, align_bytes=64, name="h")
                 engine.tensor_tensor(
-                    out=h[:],
-                    in0=y_of[c][:, blocks, :].rearrange("p t b -> p b t"),
-                    in1=t_of[c][:, blocks, :].rearrange("p t b -> p b t"),
+                    out=h[:].rearrange("p (r i) t -> p r i t", i=RUN),
+                    in0=y_of[c][:, g].rearrange("p r t i -> p r i t"),
+                    in1=t_of[c][:, g].rearrange("p r t i -> p r i t"),
                     op=ALU.mult,
                 )
-                grouped.append(h)
-            codes_of[c] = grouped
+                codes_of[c].append(h)
 
         def quantise_hidden(c):
             grouped = codes_of[c]
@@ -260,6 +265,7 @@ def tile_autoencoder_pb_kernel(tc, h_dec1, D2_words, D2_scales, g4, b4, D3_words
 
         def second_matmul(i):
             batch = slice((i % 2) * P, (i % 2 + 1) * P)
+            acc_of[i] = []
             for j in range(D_OUT // BANK):
                 cols = slice(j * BANK, (j + 1) * BANK)
                 acc = psum_mx.tile([P, BANK], F32, tag="mx")
@@ -274,7 +280,12 @@ def tile_autoencoder_pb_kernel(tc, h_dec1, D2_words, D2_scales, g4, b4, D3_words
                         start=(g == 0),
                         stop=(g == HID_PASSES - 1),
                     )
-                nc.vector.tensor_tensor(out=out_sb[:, i, cols], in0=acc[:], in1=out_bias[:, cols], op=ALU.add)
+                acc_of[i].append(acc)
+
+        def add_bias(i):
+            for j in range(D_OUT // BANK):
+                cols = slice(j * BANK, (j + 1) * BANK)
+                nc.vector.tensor_tensor(out=out_sb[:, i, cols], in0=acc_of[i][j][:], in1=out_bias[:, cols], op=ALU.add)
 
         def finish(i):
             for j in range(D_OUT // BANK):
@@ -282,79 +293,78 @@ def tile_autoencoder_pb_kernel(tc, h_dec1, D2_words, D2_scales, g4, b4, D3_words
                 nc.scalar.activation(out=out_sb[:, i, cols], in_=out_sb[:, i, cols], func=ACT.Sigmoid)
                 nc.sync.dma_start(out=out[i * P : (i + 1) * P, cols], in_=out_sb[:, i, cols])
 
+        both = (nc.vector, nc.gpsimd)
         transpose_x(0)
+        transpose_x(1)
         quantise_x(0)
         first_matmul(0)
         first_matmul(1)
-        transpose_x(1)
         transpose_x(2)
-        statistics(0, True)
+        transpose_x(3)
+        statistics(0)
         quantise_x(1)
         first_matmul(2)
-        transpose_x(3)
-        statistics(1, False)
-        columns()
-        normalise(0)
-        statistics(2, True)
-        quantise_x(2)
+        statistics(1)
+        offset(0)
+        normalise_scalar(0)
         first_matmul(3)
-        normalise(1)
-        normalise(2)
+        columns()
+        statistics(2)
+        quantise_x(2)
+        normalise_vector(1)
+        first_matmul(4)
+        offset(2)
+        normalise_scalar(2)
+        statistics(3)
         mish_sigmoid(0, 0)
         mish_sigmoid(0, 1)
-        first_matmul(4)
-        statistics(3, False)
-        mish_sigmoid(0, 2)
-        statistics(4, True)
         first_matmul(5)
-        mish_sigmoid(0, 3)
-        normalise(3)
-        normalise(4)
         quantise_x(3)
-        statistics(5, False)
+        statistics(4)
+        mish_sigmoid(0, 2)
+        mish_sigmoid(0, 3)
+        normalise_vector(3)
+        first_matmul(6)
+        offset(4)
+        normalise_scalar(4)
+        statistics(5)
         mish_sigmoid(1, 0)
         mish_sigmoid(1, 1)
-        first_matmul(6)
-        statistics(6, True)
-        mish_sigmoid(1, 2)
         first_matmul(7)
+        statistics(6)
+        mish_sigmoid(1, 2)
         mish_sigmoid(1, 3)
-        normalise(5)
-        normalise(6)
-        statistics(7, False)
-        for bank in range(BLOCKS // 2):
-            mish_sigmoid(2, bank)
-        normalise(7)
+        normalise_vector(5)
+        offset(6)
+        normalise_scalar(6)
+        statistics(7)
+        mish_sigmoid(2, 0)
+        mish_sigmoid(2, 1)
+        offset(7)
+        normalise_scalar(7)
+        mish_sigmoid(2, 2)
+        mish_sigmoid(2, 3)
         for bank in range(BLOCKS // 2):
             mish_sigmoid(3, bank)
+            affine(0, bank)
         for c in range(TILES // 2):
             mish_ln(c)
-            affine(c)
+        for c in range(1, TILES // 2):
+            for bank in range(BLOCKS // 2):
+                affine(c, bank)
         mish_tanh(0)
-        multiply_hidden(0, nc.vector)
+        multiply_hidden(0, (nc.vector, nc.vector))
         quantise_hidden(0)
-        mish_tanh(1)
-        multiply_hidden(1, nc.gpsimd)
-        mish_tanh(2)
-        multiply_hidden(2, nc.gpsimd)
-        second_matmul(0)
-        second_matmul(1)
-        finish(0)
-        finish(1)
-        mish_tanh(3)
-        quantise_hidden(1)
-        second_matmul(2)
-        multiply_hidden(3, nc.vector)
-        quantise_hidden(3)
-        second_matmul(3)
-        finish(2)
-        finish(3)
-        second_matmul(6)
-        second_matmul(7)
-        finish(6)
-        finish(7)
-        quantise_hidden(2)
-        second_matmul(4)
-        second_matmul(5)
-        finish(4)
-        finish(5)
+        for c in range(TILES // 2):
+            if c == 0:
+                mish_tanh(1)
+            if c < 2:
+                mish_tanh(c + 2)
+            if c < 3:
+                multiply_hidden(c + 1, both)
+            for i in (2 * c, 2 * c + 1):
+                second_matmul(i)
+                add_bias(i)
+                finish(i)
+            if c < 3:
+                quantise_hidden(c + 1)

@@ -65,9 +65,12 @@ def tile_autoencoder_pb_kernel(tc, h_dec1, D2_words, D2_scales, g4, b4, D3_words
                 out=d2_plane[32 * quad : 32 * quad + 4, :].bitcast(I32),
                 in_=D2_scales[0, 4 * quad : 4 * quad + 4, :].bitcast(I32),
             )
-        nc.sync.dma_start(
-            out=w2_words[:].bitcast(I32), in_=D2_words[0].rearrange("p n t -> p (n t)").bitcast(I32)
-        )
+        d2_rows = D2_words[0].rearrange("p n t -> p (n t)")
+        for j in range(HID_BANKS):
+            nc.sync.dma_start(
+                out=w2_words[:, j * BANK : (j + 1) * BANK].bitcast(I32),
+                in_=d2_rows[:, j * BANK * PACK : (j + 1) * BANK * PACK].bitcast(I32),
+            )
         nc.sync.dma_start(out=x_sb[:, 2:4, :], in_=x_rows[:, 2:4, :])
         gain_bf = keep.tile([P, BLOCKS], BF16)
         shift_bf = keep.tile([P, BLOCKS], BF16)
@@ -125,6 +128,7 @@ def tile_autoencoder_pb_kernel(tc, h_dec1, D2_words, D2_scales, g4, b4, D3_words
             nc.vector.quantize_mx(out=x_codes[:, cols].bitcast(FP8X4), scales=x_scales[:, cols], in_=x_pair(c))
 
         u_of = {}
+        bn_of = {}
         stats_of = {}
         offset_of = {}
         z_of = {}
@@ -154,6 +158,10 @@ def tile_autoencoder_pb_kernel(tc, h_dec1, D2_words, D2_scales, g4, b4, D3_words
             stats = small.tile([P, HID_BANKS, 6], F32)
             for j in range(HID_BANKS):
                 nc.vector.bn_stats(out=stats[:, j, :], in_=u_of[i][j][:])
+            bn_of[i] = stats
+
+        def deviation(i):
+            stats = bn_of[i]
             mean_var = small.tile([P, 2], F32)
             nc.vector.bn_aggr(out=mean_var[:], in_=stats[:].rearrange("p j s -> p (j s)"))
             var_eps = small.tile([P, 1], F32)
@@ -243,9 +251,9 @@ def tile_autoencoder_pb_kernel(tc, h_dec1, D2_words, D2_scales, g4, b4, D3_words
             for g, engine in enumerate(engines):
                 h = work.tile([P, 2 * P, PACK], BF16, align_bytes=64, name="h")
                 engine.tensor_tensor(
-                    out=h[:].rearrange("p (r i) t -> p r i t", i=RUN),
-                    in0=y_of[c][:, g].rearrange("p r t i -> p r i t"),
-                    in1=t_of[c][:, g].rearrange("p r t i -> p r i t"),
+                    out=h[:].rearrange("p (r i) t -> p r t i", i=RUN),
+                    in0=y_of[c][:, g],
+                    in1=t_of[c][:, g],
                     op=ALU.mult,
                 )
                 codes_of[c].append(h)
@@ -293,7 +301,6 @@ def tile_autoencoder_pb_kernel(tc, h_dec1, D2_words, D2_scales, g4, b4, D3_words
                 nc.scalar.activation(out=out_sb[:, i, cols], in_=out_sb[:, i, cols], func=ACT.Sigmoid)
                 nc.sync.dma_start(out=out[i * P : (i + 1) * P, cols], in_=out_sb[:, i, cols])
 
-        both = (nc.vector, nc.gpsimd)
         transpose_x(0)
         transpose_x(1)
         quantise_x(0)
@@ -304,46 +311,52 @@ def tile_autoencoder_pb_kernel(tc, h_dec1, D2_words, D2_scales, g4, b4, D3_words
         statistics(0)
         quantise_x(1)
         first_matmul(2)
+        deviation(0)
         statistics(1)
+        columns()
         offset(0)
+        deviation(1)
         normalise_scalar(0)
         first_matmul(3)
-        columns()
         statistics(2)
         quantise_x(2)
-        normalise_vector(1)
+        offset(1)
+        deviation(2)
+        normalise_scalar(1)
         first_matmul(4)
-        offset(2)
-        normalise_scalar(2)
         statistics(3)
+        quantise_x(3)
+        offset(2)
+        deviation(3)
+        normalise_scalar(2)
         mish_sigmoid(0, 0)
         mish_sigmoid(0, 1)
         first_matmul(5)
-        quantise_x(3)
         statistics(4)
+        offset(3)
+        deviation(4)
+        normalise_scalar(3)
         mish_sigmoid(0, 2)
         mish_sigmoid(0, 3)
-        normalise_vector(3)
         first_matmul(6)
-        offset(4)
-        normalise_scalar(4)
         statistics(5)
+        normalise_vector(4)
+        deviation(5)
         mish_sigmoid(1, 0)
         mish_sigmoid(1, 1)
         first_matmul(7)
-        statistics(6)
         mish_sigmoid(1, 2)
         mish_sigmoid(1, 3)
+        statistics(6)
         normalise_vector(5)
-        offset(6)
-        normalise_scalar(6)
+        deviation(6)
         statistics(7)
-        mish_sigmoid(2, 0)
-        mish_sigmoid(2, 1)
-        offset(7)
-        normalise_scalar(7)
-        mish_sigmoid(2, 2)
-        mish_sigmoid(2, 3)
+        offset(6)
+        deviation(7)
+        normalise_scalar(6)
+        for bank in range(BLOCKS // 2):
+            mish_sigmoid(2, bank)
+        normalise_vector(7)
         for bank in range(BLOCKS // 2):
             mish_sigmoid(3, bank)
             affine(0, bank)
@@ -361,7 +374,7 @@ def tile_autoencoder_pb_kernel(tc, h_dec1, D2_words, D2_scales, g4, b4, D3_words
             if c < 2:
                 mish_tanh(c + 2)
             if c < 3:
-                multiply_hidden(c + 1, both)
+                multiply_hidden(c + 1, (nc.vector, nc.gpsimd))
             for i in (2 * c, 2 * c + 1):
                 second_matmul(i)
                 add_bias(i)

@@ -59,7 +59,8 @@ def tile_autoencoder_pb_kernel(tc, h_dec1, D2_words, D2_scales, g4, b4, D3_words
         x_rows = h_dec1.rearrange("(i p) k -> p i k", p=P)
         w2_words = keep.tile([P, D_HID], U32, align_bytes=64)
         w3_words = keep.tile([P, HID_PASSES, D_OUT], U32, align_bytes=64)
-        nc.sync.dma_start(out=x_sb[:, 0:2, :], in_=x_rows[:, 0:2, :])
+        for i in range(2):
+            nc.sync.dma_start(out=x_sb[:, i, :], in_=x_rows[:, i, :])
         for quad in range(4):
             nc.sync.dma_start(
                 out=d2_plane[32 * quad : 32 * quad + 4, :].bitcast(I32),
@@ -109,23 +110,25 @@ def tile_autoencoder_pb_kernel(tc, h_dec1, D2_words, D2_scales, g4, b4, D3_words
         x_codes = keep.tile([P, TILES * P], U32, align_bytes=64)
         x_scales = keep.tile([P, TILES * P], U8, align_bytes=64)
 
-        def x_pair(c):
-            return x_grouped[:, 2 * c : 2 * c + 2, :, :].rearrange("p i b t -> p (i b t)")
+        def x_tiles(first, count):
+            return x_grouped[:, first : first + count, :, :].rearrange("p i b t -> p (i b t)")
 
-        def transpose_x(c):
-            x_t = psum_tr.tile([P, 2, 2, P], F32, tag="tr")
-            for i in range(2):
-                words = x_sb[:, 2 * c + i, :].bitcast(F32)
+        def transpose_x(first, count):
+            x_t = psum_tr.tile([P, count, 2, P], F32, tag="tr")
+            for i in range(count):
+                words = x_sb[:, first + i, :].bitcast(F32)
                 for half in range(2):
                     nc.tensor.transpose(x_t[:, i, half, :], words[:, half : D_IN // 2 : 2], ident[:])
             nc.scalar.copy(
-                out=x_pair(c).bitcast(F32).rearrange("p (i b h) -> p i b h", i=2, h=2),
+                out=x_tiles(first, count).bitcast(F32).rearrange("p (i b h) -> p i b h", i=count, h=2),
                 in_=x_t[:].rearrange("p i h b -> p i b h"),
             )
 
-        def quantise_x(c):
-            cols = slice(2 * c * P, (2 * c + 2) * P)
-            nc.vector.quantize_mx(out=x_codes[:, cols].bitcast(FP8X4), scales=x_scales[:, cols], in_=x_pair(c))
+        def quantise_x(first, count):
+            cols = slice(first * P, (first + count) * P)
+            nc.vector.quantize_mx(
+                out=x_codes[:, cols].bitcast(FP8X4), scales=x_scales[:, cols], in_=x_tiles(first, count)
+            )
 
         u_of = {}
         bn_of = {}
@@ -301,31 +304,33 @@ def tile_autoencoder_pb_kernel(tc, h_dec1, D2_words, D2_scales, g4, b4, D3_words
                 nc.scalar.activation(out=out_sb[:, i, cols], in_=out_sb[:, i, cols], func=ACT.Sigmoid)
                 nc.sync.dma_start(out=out[i * P : (i + 1) * P, cols], in_=out_sb[:, i, cols])
 
-        transpose_x(0)
-        transpose_x(1)
-        quantise_x(0)
+        transpose_x(0, 1)
+        transpose_x(1, 1)
+        quantise_x(0, 1)
         first_matmul(0)
+        quantise_x(1, 1)
         first_matmul(1)
-        transpose_x(2)
-        transpose_x(3)
+        transpose_x(2, 2)
+        transpose_x(4, 2)
+        transpose_x(6, 2)
         statistics(0)
-        quantise_x(1)
-        first_matmul(2)
         deviation(0)
         statistics(1)
-        columns()
         offset(0)
+        quantise_x(2, 2)
+        first_matmul(2)
         deviation(1)
         normalise_scalar(0)
         first_matmul(3)
         statistics(2)
-        quantise_x(2)
+        quantise_x(4, 2)
         offset(1)
         deviation(2)
+        columns()
         normalise_scalar(1)
         first_matmul(4)
         statistics(3)
-        quantise_x(3)
+        quantise_x(6, 2)
         offset(2)
         deviation(3)
         normalise_scalar(2)
@@ -351,9 +356,8 @@ def tile_autoencoder_pb_kernel(tc, h_dec1, D2_words, D2_scales, g4, b4, D3_words
         normalise_vector(5)
         deviation(6)
         statistics(7)
-        offset(6)
+        normalise_vector(6)
         deviation(7)
-        normalise_scalar(6)
         for bank in range(BLOCKS // 2):
             mish_sigmoid(2, bank)
         normalise_vector(7)

@@ -356,10 +356,10 @@ def tile_autoencoder_pb_kernel(tc, h_dec1, D2_words, D2_scales, g4, b4, D3_words
         normalise_vector(5)
         deviation(6)
         statistics(7)
-        normalise_vector(6)
-        deviation(7)
         for bank in range(BLOCKS // 2):
             mish_sigmoid(2, bank)
+        deviation(7)
+        normalise_vector(6)
         normalise_vector(7)
         for bank in range(BLOCKS // 2):
             mish_sigmoid(3, bank)
@@ -379,9 +379,11 @@ def tile_autoencoder_pb_kernel(tc, h_dec1, D2_words, D2_scales, g4, b4, D3_words
                 mish_tanh(c + 2)
             if c < 3:
                 multiply_hidden(c + 1, (nc.vector, nc.gpsimd))
-            for i in (2 * c, 2 * c + 1):
-                second_matmul(i)
-                add_bias(i)
-                finish(i)
+            second_matmul(2 * c)
+            second_matmul(2 * c + 1)
+            add_bias(2 * c)
+            finish(2 * c)
             if c < 3:
                 quantise_hidden(c + 1)
+            add_bias(2 * c + 1)
+            finish(2 * c + 1)

@@ -25,6 +25,10 @@ BLOCKS = D_HID // P
 RUN = 4
 RUNS = 2 * P // RUN
 EPS = 1e-5
+RUN = 4
+RUNS = 2 * P // RUN
+HALF = 2 * P * PACK
+RATIONAL = HALF // 2
 LN_FLOOR = 2.0**-60
 
 FLOPS = 2 * BATCH * D_IN * D_HID + 2 * BATCH * D_HID * D_OUT
@@ -37,7 +41,9 @@ def tile_autoencoder_pb_kernel(tc, h_dec1, D2_words, D2_scales, g4, b4, D3_words
         keep = stack.enter_context(tc.tile_pool(name="keep", bufs=1))
         small = stack.enter_context(tc.tile_pool(name="small", bufs=TILES))
         rows = stack.enter_context(tc.tile_pool(name="rows", bufs=TILES))
+        quads = stack.enter_context(tc.tile_pool(name="quads", bufs=TILES // 4))
         pairs = stack.enter_context(tc.tile_pool(name="pairs", bufs=TILES // 2))
+        hidden = stack.enter_context(tc.tile_pool(name="hidden", bufs=2))
         work = stack.enter_context(tc.tile_pool(name="work", bufs=4))
         psum_mx = stack.enter_context(tc.psum_pool(name="psum_mx", bufs=6))
         psum_tr = stack.enter_context(tc.psum_pool(name="psum_tr", bufs=2))
@@ -72,7 +78,7 @@ def tile_autoencoder_pb_kernel(tc, h_dec1, D2_words, D2_scales, g4, b4, D3_words
                 out=w2_words[:, j * BANK : (j + 1) * BANK].bitcast(I32),
                 in_=d2_rows[:, j * BANK * PACK : (j + 1) * BANK * PACK].bitcast(I32),
             )
-        nc.sync.dma_start(out=x_sb[:, 2:4, :], in_=x_rows[:, 2:4, :])
+            nc.sync.dma_start(out=x_sb[:, 2 + j, :], in_=x_rows[:, 2 + j, :])
         gain_bf = keep.tile([P, BLOCKS], BF16)
         shift_bf = keep.tile([P, BLOCKS], BF16)
         for column, vector in ((gain_bf, g4), (shift_bf, b4)):
@@ -102,9 +108,7 @@ def tile_autoencoder_pb_kernel(tc, h_dec1, D2_words, D2_scales, g4, b4, D3_words
         def columns():
             for plain, minus, column in ((gain, minus_gain, gain_bf), (shift, minus_shift, shift_bf)):
                 nc.vector.tensor_copy(out=plain[:], in_=column[:])
-                nc.vector.tensor_scalar(
-                    out=minus[:], in0=column[:], scalar1=-1.0, scalar2=None, op0=ALU.mult
-                )
+                nc.vector.tensor_scalar(out=minus[:], in0=column[:], scalar1=-1.0, scalar2=None, op0=ALU.mult)
 
         x_grouped = keep.tile([P, TILES, P, PACK], BF16, align_bytes=64)
         x_codes = keep.tile([P, TILES * P], U32, align_bytes=64)
@@ -137,6 +141,7 @@ def tile_autoencoder_pb_kernel(tc, h_dec1, D2_words, D2_scales, g4, b4, D3_words
         z_of = {}
         y_of = {}
         t_of = {}
+        h_of = {}
         codes_of = {}
         acc_of = {}
 
@@ -205,8 +210,8 @@ def tile_autoencoder_pb_kernel(tc, h_dec1, D2_words, D2_scales, g4, b4, D3_words
                     out=z, in0=u, scalar1=mean_var[:, 0:1], scalar2=rstd[:], op0=ALU.subtract, op1=ALU.mult
                 )
 
-        def turn(c, bank, pool, tag):
-            z_t = pool.tile([P, 2, 2 * P], F32, tag=tag, name="z_t")
+        def turn(c, bank):
+            z_t = psum_tr.tile([P, 2, 2 * P], F32, tag="tr", name="z_t")
             for b in range(2):
                 for i in range(2):
                     cols = slice((2 * bank + b) * P, (2 * bank + b + 1) * P)
@@ -216,7 +221,7 @@ def tile_autoencoder_pb_kernel(tc, h_dec1, D2_words, D2_scales, g4, b4, D3_words
         def mish_sigmoid(c, bank):
             if bank == 0:
                 t_of[c] = pairs.tile([P, HID_PASSES, RUNS, PACK, RUN], F32, name="t")
-            z_t = turn(c, bank, psum_tr, "tr")
+            z_t = turn(c, bank)
             for b in range(2):
                 block = 2 * bank + b
                 nc.scalar.activation(
@@ -227,50 +232,66 @@ def tile_autoencoder_pb_kernel(tc, h_dec1, D2_words, D2_scales, g4, b4, D3_words
                     bias=minus_shift[:, block : block + 1],
                 )
 
-        def affine(c, bank):
-            if bank == 0:
-                y_of[c] = pairs.tile([P, HID_PASSES, RUNS, PACK, RUN], F32, name="y")
-            z_t = turn(c, bank, psum_mx, "mx")
-            for b in range(2):
-                block = 2 * bank + b
-                nc.vector.tensor_scalar(
-                    out=y_of[c][:, block // PACK, :, block % PACK, :],
-                    in0=z_t[:, b, :].rearrange("p (r i) -> p r i", i=RUN),
-                    scalar1=gain[:, block : block + 1],
-                    scalar2=shift[:, block : block + 1],
-                    op0=ALU.mult,
-                    op1=ALU.add,
-                )
+        def affine(q, block):
+            if block == 0:
+                y_of[q] = quads.tile([P, HID_PASSES, 2 * RUNS, PACK, RUN], F32, name="y")
+            z_t = psum_mx.tile([P, BANK], F32, tag="mx", name="z_t")
+            for i in range(4):
+                cols = slice(block * P, (block + 1) * P)
+                nc.tensor.transpose(z_t[:, i * P : (i + 1) * P], z_of[4 * q + i][:, cols], ident[:])
+            nc.vector.tensor_scalar(
+                out=y_of[q][:, block // PACK, :, block % PACK, :],
+                in0=z_t[:].rearrange("p (r i) -> p r i", i=RUN),
+                scalar1=gain[:, block : block + 1],
+                scalar2=shift[:, block : block + 1],
+                op0=ALU.mult,
+                op1=ALU.add,
+            )
+
+        def columns_of(c, first, last):
+            return t_of[c][:].rearrange("p g r t i -> p (g r t i)")[:, first:last]
+
+        def rational_start():
+            s = columns_of(0, 0, RATIONAL)
+            nc.gpsimd.tensor_tensor(out=s, in0=s, in1=s, op=ALU.mult)
+            nc.gpsimd.tensor_scalar(out=s, in0=s, scalar1=1.0, scalar2=1.0, op0=ALU.mult, op1=ALU.add)
+
+        def rational_end():
+            s = columns_of(0, 0, RATIONAL)
+            nc.vector.reciprocal(out=s, in_=s)
+            nc.vector.tensor_scalar(out=s, in0=s, scalar1=2.0, scalar2=-1.0, op0=ALU.mult, op1=ALU.add)
 
         def mish_ln(c):
-            nc.scalar.activation(out=t_of[c][:], in_=t_of[c][:], func=ACT.Ln, bias=ln_floor[:])
+            t = columns_of(c, RATIONAL if c == 0 else 0, HID_PASSES * HALF)
+            nc.scalar.activation(out=t, in_=t, func=ACT.Ln, bias=ln_floor[:])
 
         def mish_tanh(c):
             for g in range(HID_PASSES):
-                nc.scalar.activation(out=t_of[c][:, g], in_=t_of[c][:, g], func=ACT.Tanh, scale=-1.0)
+                t = columns_of(c, RATIONAL if c == g == 0 else g * HALF, (g + 1) * HALF)
+                nc.scalar.activation(out=t, in_=t, func=ACT.Tanh, scale=-1.0)
 
-        def multiply_hidden(c, engines):
-            codes_of[c] = []
-            for g, engine in enumerate(engines):
-                h = work.tile([P, 2 * P, PACK], BF16, align_bytes=64, name="h")
-                engine.tensor_tensor(
-                    out=h[:].rearrange("p (r i) t -> p r t i", i=RUN),
-                    in0=y_of[c][:, g],
-                    in1=t_of[c][:, g],
-                    op=ALU.mult,
-                )
-                codes_of[c].append(h)
+        def multiply_hidden(c, engine, first, last):
+            if c not in h_of:
+                h_of[c] = hidden.tile([P, HID_PASSES * 2 * P, PACK], BF16, align_bytes=64, name="h")
+            for g in range(HID_PASSES):
+                a, b = max(first, g * RUNS), min(last, (g + 1) * RUNS)
+                if a < b:
+                    runs = slice(a - g * RUNS, b - g * RUNS)
+                    engine.tensor_tensor(
+                        out=h_of[c][:].rearrange("p (r i) t -> p r t i", i=RUN)[:, a:b],
+                        in0=y_of[c // 2][:, g, c % 2 * RUNS + a - g * RUNS : c % 2 * RUNS + b - g * RUNS],
+                        in1=t_of[c][:, g, runs],
+                        op=ALU.mult,
+                    )
 
         def quantise_hidden(c):
-            grouped = codes_of[c]
-            codes_of[c] = []
-            for h in grouped:
+            codes_of[c] = {}
+            for g in reversed(range(HID_PASSES)):
                 codes = work.tile([P, 2 * P], U32, align_bytes=64, name="codes")
                 scales = work.tile([P, 2 * P], U8, align_bytes=64, name="scales")
-                nc.vector.quantize_mx(
-                    out=codes[:].bitcast(FP8X4), scales=scales[:], in_=h[:].rearrange("p b t -> p (b t)")
-                )
-                codes_of[c].append((codes, scales))
+                h = h_of[c][:, g * 2 * P : (g + 1) * 2 * P, :]
+                nc.vector.quantize_mx(out=codes[:].bitcast(FP8X4), scales=scales[:], in_=h.rearrange("p b t -> p (b t)"))
+                codes_of[c][g] = (codes, scales)
 
         out_sb = keep.tile([P, TILES, D_OUT], F32)
 
@@ -310,29 +331,31 @@ def tile_autoencoder_pb_kernel(tc, h_dec1, D2_words, D2_scales, g4, b4, D3_words
         first_matmul(0)
         quantise_x(1, 1)
         first_matmul(1)
-        transpose_x(2, 2)
-        transpose_x(4, 2)
-        transpose_x(6, 2)
+        transpose_x(2, 1)
+        transpose_x(3, 1)
         statistics(0)
         deviation(0)
         statistics(1)
-        offset(0)
-        quantise_x(2, 2)
+        quantise_x(2, 1)
         first_matmul(2)
+        offset(0)
+        quantise_x(3, 1)
         deviation(1)
         normalise_scalar(0)
+        transpose_x(4, 2)
         first_matmul(3)
         statistics(2)
-        quantise_x(4, 2)
         offset(1)
         deviation(2)
+        quantise_x(4, 2)
         columns()
         normalise_scalar(1)
+        transpose_x(6, 2)
         first_matmul(4)
         statistics(3)
-        quantise_x(6, 2)
         offset(2)
         deviation(3)
+        quantise_x(6, 2)
         normalise_scalar(2)
         mish_sigmoid(0, 0)
         mish_sigmoid(0, 1)
@@ -364,21 +387,25 @@ def tile_autoencoder_pb_kernel(tc, h_dec1, D2_words, D2_scales, g4, b4, D3_words
         for bank in range(BLOCKS // 2):
             mish_sigmoid(3, bank)
             affine(0, bank)
+        rational_start()
         for c in range(TILES // 2):
             mish_ln(c)
-        for c in range(1, TILES // 2):
-            for bank in range(BLOCKS // 2):
-                affine(c, bank)
+        for q, block in [(0, block) for block in range(BLOCKS // 2, BLOCKS)] + [(1, block) for block in range(BLOCKS)]:
+            affine(q, block)
+        rational_end()
+        first_part = RATIONAL // (PACK * RUN)
+        multiply_hidden(0, nc.vector, 0, first_part)
         mish_tanh(0)
-        multiply_hidden(0, (nc.vector, nc.vector))
+        multiply_hidden(0, nc.vector, first_part, RUNS)
+        multiply_hidden(0, nc.vector, RUNS, HID_PASSES * RUNS)
         quantise_hidden(0)
+        mish_tanh(1)
         for c in range(TILES // 2):
-            if c == 0:
-                mish_tanh(1)
             if c < 2:
                 mish_tanh(c + 2)
             if c < 3:
-                multiply_hidden(c + 1, (nc.vector, nc.gpsimd))
+                multiply_hidden(c + 1, nc.vector, 0, RUNS)
+                multiply_hidden(c + 1, nc.gpsimd, RUNS, HID_PASSES * RUNS)
             second_matmul(2 * c)
             second_matmul(2 * c + 1)
             add_bias(2 * c)

from contextlib import ExitStack

import concourse.mybir as mybir
from concourse.masks import make_identity

F32 = mybir.dt.float32
BF16 = mybir.dt.bfloat16
I32 = mybir.dt.int32
U32 = mybir.dt.uint32
U8 = mybir.dt.uint8
FP8X4 = mybir.dt.float8_e4m3fn_x4
ACT = mybir.ActivationFunctionType
ALU = mybir.AluOpType

P = 128
PACK = 4
K_PASS = P * PACK
BANK = 512

BATCH, D_IN, D_HID, D_OUT = 1024, 512, 1024, 1536
TILES = BATCH // P
HID_BANKS = D_HID // BANK
HID_PASSES = D_HID // K_PASS
BLOCKS = D_HID // P
RUN = 4
RUNS = 2 * P // RUN
EPS = 1e-5
RUN = 4
RUNS = 2 * P // RUN
HALF = 2 * P * PACK
RATIONAL = HALF // 2
LN_FLOOR = 2.0**-60

FLOPS = 2 * BATCH * D_IN * D_HID + 2 * BATCH * D_HID * D_OUT


def tile_autoencoder_pb_kernel(tc, h_dec1, D2_words, D2_scales, g4, b4, D3_words, D3_scales, bo, out):
    nc = tc.nc
    with ExitStack() as stack:
        stack.enter_context(tc.manual_schedule())
        keep = stack.enter_context(tc.tile_pool(name="keep", bufs=1))
        small = stack.enter_context(tc.tile_pool(name="small", bufs=TILES))
        rows = stack.enter_context(tc.tile_pool(name="rows", bufs=TILES))
        quads = stack.enter_context(tc.tile_pool(name="quads", bufs=TILES // 4))
        pairs = stack.enter_context(tc.tile_pool(name="pairs", bufs=TILES // 2))
        hidden = stack.enter_context(tc.tile_pool(name="hidden", bufs=2))
        work = stack.enter_context(tc.tile_pool(name="work", bufs=4))
        psum_mx = stack.enter_context(tc.psum_pool(name="psum_mx", bufs=6))
        psum_tr = stack.enter_context(tc.psum_pool(name="psum_tr", bufs=2))

        d2_plane = keep.tile([P, D_HID], U8, align_bytes=64)
        nc.vector.memset(d2_plane[:].bitcast(I32), 0)
        planes = keep.tile([P, D_OUT], U8, align_bytes=64)
        nc.vector.memset(planes[:].bitcast(I32), 0)
        ln_floor = keep.tile([P, 1], F32)
        nc.vector.memset(ln_floor[:], LN_FLOOR)
        minus_half = keep.tile([P, 1], F32)
        nc.vector.memset(minus_half[:], -0.5)
        ident = keep.tile([P, P], F32)
        make_identity(nc, ident[:])
        warm = keep.tile([P, 1], F32)
        nc.scalar.activation(out=warm[:], in_=ln_floor[:], func=ACT.Sigmoid)

        x_sb = keep.tile([P, TILES, D_IN], BF16)
        x_rows = h_dec1.rearrange("(i p) k -> p i k", p=P)
        w2_words = keep.tile([P, D_HID], U32, align_bytes=64)
        w3_words = keep.tile([P, HID_PASSES, D_OUT], U32, align_bytes=64)
        for i in range(2):
            nc.sync.dma_start(out=x_sb[:, i, :], in_=x_rows[:, i, :])
        for quad in range(4):
            nc.sync.dma_start(
                out=d2_plane[32 * quad : 32 * quad + 4, :].bitcast(I32),
                in_=D2_scales[0, 4 * quad : 4 * quad + 4, :].bitcast(I32),
            )
        d2_rows = D2_words[0].rearrange("p n t -> p (n t)")
        for j in range(HID_BANKS):
            nc.sync.dma_start(
                out=w2_words[:, j * BANK : (j + 1) * BANK].bitcast(I32),
                in_=d2_rows[:, j * BANK * PACK : (j + 1) * BANK * PACK].bitcast(I32),
            )
            nc.sync.dma_start(out=x_sb[:, 2 + j, :], in_=x_rows[:, 2 + j, :])
        gain_bf = keep.tile([P, BLOCKS], BF16)
        shift_bf = keep.tile([P, BLOCKS], BF16)
        for column, vector in ((gain_bf, g4), (shift_bf, b4)):
            nc.scalar.dma_start(
                out=column[:].rearrange("p (g t) -> p g t", t=PACK),
                in_=vector.rearrange("(g p t) -> p g t", p=P, t=PACK),
            )
        nc.sync.dma_start(out=x_sb[:, 4:TILES, :], in_=x_rows[:, 4:TILES, :])
        for quad in range(4):
            nc.sync.dma_start(
                out=planes[32 * quad : 32 * quad + 4 * HID_PASSES, :].bitcast(I32),
                in_=D3_scales[:, 4 * quad : 4 * quad + 4, :].bitcast(I32),
            )
        for g in range(HID_PASSES):
            nc.sync.dma_start(
                out=w3_words[:, g, :].bitcast(I32),
                in_=D3_words[g].rearrange("p n t -> p (n t)").bitcast(I32),
            )
        out_bias = keep.tile([P, D_OUT], BF16)
        nc.sync.dma_start(out=out_bias[:], in_=bo.partition_broadcast(P))

        gain = keep.tile([P, BLOCKS], F32)
        shift = keep.tile([P, BLOCKS], F32)
        minus_gain = keep.tile([P, BLOCKS], F32)
        minus_shift = keep.tile([P, BLOCKS], F32)

        def columns():
            for plain, minus, column in ((gain, minus_gain, gain_bf), (shift, minus_shift, shift_bf)):
                nc.vector.tensor_copy(out=plain[:], in_=column[:])
                nc.vector.tensor_scalar(out=minus[:], in0=column[:], scalar1=-1.0, scalar2=None, op0=ALU.mult)

        x_grouped = keep.tile([P, TILES, P, PACK], BF16, align_bytes=64)
        x_codes = keep.tile([P, TILES * P], U32, align_bytes=64)
        x_scales = keep.tile([P, TILES * P], U8, align_bytes=64)

        def x_tiles(first, count):
            return x_grouped[:, first : first + count, :, :].rearrange("p i b t -> p (i b t)")

        def transpose_x(first, count):
            x_t = psum_tr.tile([P, count, 2, P], F32, tag="tr")
            for i in range(count):
                words = x_sb[:, first + i, :].bitcast(F32)
                for half in range(2):
                    nc.tensor.transpose(x_t[:, i, half, :], words[:, half : D_IN // 2 : 2], ident[:])
            nc.scalar.copy(
                out=x_tiles(first, count).bitcast(F32).rearrange("p (i b h) -> p i b h", i=count, h=2),
                in_=x_t[:].rearrange("p i h b -> p i b h"),
            )

        def quantise_x(first, count):
            cols = slice(first * P, (first + count) * P)
            nc.vector.quantize_mx(
                out=x_codes[:, cols].bitcast(FP8X4), scales=x_scales[:, cols], in_=x_tiles(first, count)
            )

        u_of = {}
        bn_of = {}
        stats_of = {}
        offset_of = {}
        z_of = {}
        y_of = {}
        t_of = {}
        h_of = {}
        codes_of = {}
        acc_of = {}

        def first_matmul(i):
            batch = slice(i * P, (i + 1) * P)
            u_of[i] = []
            for j in range(HID_BANKS):
                cols = slice(j * BANK, (j + 1) * BANK)
                u = psum_mx.tile([P, BANK], F32, tag="mx")
                nc.tensor.matmul_mx(
                    out=u[:],
                    lhsT=x_codes[:, batch].bitcast(FP8X4),
                    lhsT_scale=x_scales[:, batch],
                    rhs=w2_words[:, cols].bitcast(FP8X4),
                    rhs_scale=d2_plane[:, cols],
                    start=True,
                    stop=True,
                )
                u_of[i].append(u)

        def statistics(i):
            stats = small.tile([P, HID_BANKS, 6], F32)
            for j in range(HID_BANKS):
                nc.vector.bn_stats(out=stats[:, j, :], in_=u_of[i][j][:])
            bn_of[i] = stats

        def deviation(i):
            stats = bn_of[i]
            mean_var = small.tile([P, 2], F32)
            nc.vector.bn_aggr(out=mean_var[:], in_=stats[:].rearrange("p j s -> p (j s)"))
            var_eps = small.tile([P, 1], F32)
            nc.gpsimd.tensor_scalar(
                out=var_eps[:], in0=mean_var[:, 1:2], scalar1=1.0, scalar2=EPS, op0=ALU.mult, op1=ALU.add
            )
            rstd = small.tile([P, 1], F32)
            nc.gpsimd.tensor_tensor(out=rstd[:], in0=var_eps[:], in1=minus_half[:], op=ALU.pow)
            stats_of[i] = (mean_var, rstd)

        def z_views(i, j):
            return (
                z_of[i][:, j * BANK : (j + 1) * BANK].rearrange("p (t q) -> p t q", t=PACK),
                u_of[i][j][:].rearrange("p (q t) -> p t q", t=PACK),
            )

        def offset(i):
            mean_var, rstd = stats_of[i]
            offset_of[i] = small.tile([P, 1], F32, name="minus_mean_rstd")
            nc.vector.scalar_tensor_tensor(
                out=offset_of[i][:], in0=mean_var[:, 0:1], scalar=-1.0, in1=rstd[:], op0=ALU.mult, op1=ALU.mult
            )

        def normalise_scalar(i):
            z_of[i] = rows.tile([P, D_HID], F32, name="z")
            for j in range(HID_BANKS):
                z, u = z_views(i, j)
                nc.scalar.activation(
                    out=z, in_=u, func=ACT.Identity, scale=stats_of[i][1][:], bias=offset_of[i][:]
                )

        def normalise_vector(i):
            mean_var, rstd = stats_of[i]
            z_of[i] = rows.tile([P, D_HID], F32, name="z")
            for j in range(HID_BANKS):
                z, u = z_views(i, j)
                nc.vector.tensor_scalar(
                    out=z, in0=u, scalar1=mean_var[:, 0:1], scalar2=rstd[:], op0=ALU.subtract, op1=ALU.mult
                )

        def turn(c, bank):
            z_t = psum_tr.tile([P, 2, 2 * P], F32, tag="tr", name="z_t")
            for b in range(2):
                for i in range(2):
                    cols = slice((2 * bank + b) * P, (2 * bank + b + 1) * P)
                    nc.tensor.transpose(z_t[:, b, i * P : (i + 1) * P], z_of[2 * c + i][:, cols], ident[:])
            return z_t

        def mish_sigmoid(c, bank):
            if bank == 0:
                t_of[c] = pairs.tile([P, HID_PASSES, RUNS, PACK, RUN], F32, name="t")
            z_t = turn(c, bank)
            for b in range(2):
                block = 2 * bank + b
                nc.scalar.activation(
                    out=t_of[c][:, block // PACK, :, block % PACK, :],
                    in_=z_t[:, b, :].rearrange("p (r i) -> p r i", i=RUN),
                    func=ACT.Sigmoid,
                    scale=minus_gain[:, block : block + 1],
                    bias=minus_shift[:, block : block + 1],
                )

        def affine(q, block):
            if block == 0:
                y_of[q] = quads.tile([P, HID_PASSES, 2 * RUNS, PACK, RUN], F32, name="y")
            z_t = psum_mx.tile([P, BANK], F32, tag="mx", name="z_t")
            for i in range(4):
                cols = slice(block * P, (block + 1) * P)
                nc.tensor.transpose(z_t[:, i * P : (i + 1) * P], z_of[4 * q + i][:, cols], ident[:])
            nc.vector.tensor_scalar(
                out=y_of[q][:, block // PACK, :, block % PACK, :],
                in0=z_t[:].rearrange("p (r i) -> p r i", i=RUN),
                scalar1=gain[:, block : block + 1],
                scalar2=shift[:, block : block + 1],
                op0=ALU.mult,
                op1=ALU.add,
            )

        def columns_of(c, first, last):
            return t_of[c][:].rearrange("p g r t i -> p (g r t i)")[:, first:last]

        def rational_start():
            s = columns_of(0, 0, RATIONAL)
            nc.gpsimd.tensor_tensor(out=s, in0=s, in1=s, op=ALU.mult)
            nc.gpsimd.tensor_scalar(out=s, in0=s, scalar1=1.0, scalar2=1.0, op0=ALU.mult, op1=ALU.add)

        def rational_end():
            s = columns_of(0, 0, RATIONAL)
            nc.vector.reciprocal(out=s, in_=s)
            nc.vector.tensor_scalar(out=s, in0=s, scalar1=2.0, scalar2=-1.0, op0=ALU.mult, op1=ALU.add)

        def mish_ln(c):
            t = columns_of(c, RATIONAL if c == 0 else 0, HID_PASSES * HALF)
            nc.scalar.activation(out=t, in_=t, func=ACT.Ln, bias=ln_floor[:])

        def mish_tanh(c):
            for g in range(HID_PASSES):
                t = columns_of(c, RATIONAL if c == g == 0 else g * HALF, (g + 1) * HALF)
                nc.scalar.activation(out=t, in_=t, func=ACT.Tanh, scale=-1.0)

        def multiply_hidden(c, engine, first, last):
            if c not in h_of:
                h_of[c] = hidden.tile([P, HID_PASSES * 2 * P, PACK], BF16, align_bytes=64, name="h")
            for g in range(HID_PASSES):
                a, b = max(first, g * RUNS), min(last, (g + 1) * RUNS)
                if a < b:
                    runs = slice(a - g * RUNS, b - g * RUNS)
                    engine.tensor_tensor(
                        out=h_of[c][:].rearrange("p (r i) t -> p r t i", i=RUN)[:, a:b],
                        in0=y_of[c // 2][:, g, c % 2 * RUNS + a - g * RUNS : c % 2 * RUNS + b - g * RUNS],
                        in1=t_of[c][:, g, runs],
                        op=ALU.mult,
                    )

        def quantise_hidden(c):
            codes_of[c] = {}
            for g in reversed(range(HID_PASSES)):
                codes = work.tile([P, 2 * P], U32, align_bytes=64, name="codes")
                scales = work.tile([P, 2 * P], U8, align_bytes=64, name="scales")
                h = h_of[c][:, g * 2 * P : (g + 1) * 2 * P, :]
                nc.vector.quantize_mx(out=codes[:].bitcast(FP8X4), scales=scales[:], in_=h.rearrange("p b t -> p (b t)"))
                codes_of[c][g] = (codes, scales)

        out_sb = keep.tile([P, TILES, D_OUT], F32)

        def second_matmul(i):
            batch = slice((i % 2) * P, (i % 2 + 1) * P)
            acc_of[i] = []
            for j in range(D_OUT // BANK):
                cols = slice(j * BANK, (j + 1) * BANK)
                acc = psum_mx.tile([P, BANK], F32, tag="mx")
                for g in range(HID_PASSES):
                    codes, scales = codes_of[i // 2][g]
                    nc.tensor.matmul_mx(
                        out=acc[:],
                        lhsT=codes[:, batch].bitcast(FP8X4),
                        lhsT_scale=scales[:, batch],
                        rhs=w3_words[:, g, cols].bitcast(FP8X4),
                        rhs_scale=planes[PACK * g : P, cols],
                        start=(g == 0),
                        stop=(g == HID_PASSES - 1),
                    )
                acc_of[i].append(acc)

        def add_bias(i):
            for j in range(D_OUT // BANK):
                cols = slice(j * BANK, (j + 1) * BANK)
                nc.vector.tensor_tensor(out=out_sb[:, i, cols], in0=acc_of[i][j][:], in1=out_bias[:, cols], op=ALU.add)

        def finish(i):
            for j in range(D_OUT // BANK):
                cols = slice(j * BANK, (j + 1) * BANK)
                nc.scalar.activation(out=out_sb[:, i, cols], in_=out_sb[:, i, cols], func=ACT.Sigmoid)
                nc.sync.dma_start(out=out[i * P : (i + 1) * P, cols], in_=out_sb[:, i, cols])

        transpose_x(0, 1)
        transpose_x(1, 1)
        quantise_x(0, 1)
        first_matmul(0)
        quantise_x(1, 1)
        first_matmul(1)
        transpose_x(2, 1)
        transpose_x(3, 1)
        statistics(0)
        deviation(0)
        statistics(1)
        quantise_x(2, 1)
        first_matmul(2)
        offset(0)
        quantise_x(3, 1)
        deviation(1)
        normalise_scalar(0)
        transpose_x(4, 2)
        first_matmul(3)
        statistics(2)
        offset(1)
        deviation(2)
        quantise_x(4, 2)
        columns()
        normalise_scalar(1)
        transpose_x(6, 2)
        first_matmul(4)
        statistics(3)
        offset(2)
        deviation(3)
        quantise_x(6, 2)
        normalise_scalar(2)
        mish_sigmoid(0, 0)
        mish_sigmoid(0, 1)
        first_matmul(5)
        statistics(4)
        offset(3)
        deviation(4)
        normalise_scalar(3)
        mish_sigmoid(0, 2)
        mish_sigmoid(0, 3)
        first_matmul(6)
        statistics(5)
        normalise_vector(4)
        deviation(5)
        mish_sigmoid(1, 0)
        mish_sigmoid(1, 1)
        first_matmul(7)
        mish_sigmoid(1, 2)
        mish_sigmoid(1, 3)
        statistics(6)
        normalise_vector(5)
        deviation(6)
        statistics(7)
        for bank in range(BLOCKS // 2):
            mish_sigmoid(2, bank)
        deviation(7)
        normalise_vector(6)
        normalise_vector(7)
        for bank in range(BLOCKS // 2):
            mish_sigmoid(3, bank)
            affine(0, bank)
        rational_start()
        for c in range(TILES // 2):
            mish_ln(c)
        for q, block in [(0, block) for block in range(BLOCKS // 2, BLOCKS)] + [(1, block) for block in range(BLOCKS)]:
            affine(q, block)
        rational_end()
        first_part = RATIONAL // (PACK * RUN)
        multiply_hidden(0, nc.vector, 0, first_part)
        mish_tanh(0)
        multiply_hidden(0, nc.vector, first_part, RUNS)
        multiply_hidden(0, nc.vector, RUNS, HID_PASSES * RUNS)
        quantise_hidden(0)
        mish_tanh(1)
        for c in range(TILES // 2):
            if c < 2:
                mish_tanh(c + 2)
            if c < 3:
                multiply_hidden(c + 1, nc.vector, 0, RUNS)
                multiply_hidden(c + 1, nc.gpsimd, RUNS, HID_PASSES * RUNS)
            second_matmul(2 * c)
            second_matmul(2 * c + 1)
            add_bias(2 * c)
            finish(2 * c)
            if c < 3:
                quantise_hidden(c + 1)
            add_bias(2 * c + 1)
            finish(2 * c + 1)
